import numpy as np
import ml_dtypes


def mxq(x, axis, fmt="e4m3"):
    dtype, down = {"e4m3": (ml_dtypes.float8_e4m3fn, 7), "e5m2": (ml_dtypes.float8_e5m2, 14)}[fmt]
    v = np.moveaxis(np.asarray(x, np.float32).astype(ml_dtypes.bfloat16).astype(np.float64), axis, -1)
    blocks = v.reshape(v.shape[:-1] + (-1, 32))
    amax = np.abs(blocks).max(-1, keepdims=True)
    byte = np.maximum(np.where(amax > 0, np.frexp(amax)[1] - 1 + 127, 0) - down, 1)
    scale = np.exp2(byte - 127.0)
    codes = (blocks / scale).astype(np.float32).astype(dtype).astype(np.float64)
    return np.moveaxis((codes * scale).reshape(v.shape), -1, axis)


WIDE = False


def mx_kscale(k):
    if not WIDE:
        return np.ones(k)
    levels = np.array([10, -10, 5, -5, 0])
    if k % 512:
        return np.exp2(np.random.permutation(np.resize(levels, k // 32))).repeat(32)
    a = np.empty((k // 512, 16))
    for p in range(k // 512):
        a[p, :8] = np.random.permutation(np.resize(levels, 8))
        for g in range(8):
            far = levels[np.abs(levels - a[p, g]) >= 10]
            a[p, g + 8] = far[np.random.randint(len(far))]
    return np.exp2(a.ravel()).repeat(32)


BF16 = ml_dtypes.bfloat16


def bf(x):
    return np.asarray(x, np.float32).astype(BF16)


def f64(x):
    return np.asarray(x).astype(np.float64)


B, N, D0, D1, D2, D3 = 32, 128, 1024, 1024, 512, 1024
EPS = 1e-5


def batch_norm(x, g, b):
    mean = x.mean(axis=(0, 1))
    var = np.square(x - mean).mean(axis=(0, 1))
    return (x - mean) * (1.0 / np.sqrt(var + EPS)) * g + b


def setup_inputs():
    s = mx_kscale(D0)
    feats = np.random.standard_normal((B, N, D0)) * np.exp(0.4 * np.random.standard_normal(D0)) + 0.5 * np.random.standard_normal(D0)
    return {"set_feats": bf(feats),
            "g0": bf((1.0 + 0.2 * np.random.standard_normal(D0)) * s),
            "b0": bf(0.2 * np.random.standard_normal(D0) * s),
            "W0": bf(np.random.standard_normal((D1, D0)) / np.sqrt(D0) / s),
            "c0": bf(0.3 * np.random.standard_normal(D1)),
            "g1": bf(1.0 + 0.2 * np.random.standard_normal(D1)),
            "b1": bf(0.2 * np.random.standard_normal(D1))}


def reference(set_feats, g0, b0, W0, c0, g1, b1):
    x0 = batch_norm(f64(set_feats), f64(g0), f64(b0))
    h0 = np.maximum((mxq(x0, 2, "e4m3") @ mxq(f64(W0), 1, "e4m3").T) + f64(c0), 0.0)
    return batch_norm(h0, f64(g1), f64(b1))

@@ -1,0 +1,344 @@
+from contextlib import ExitStack
+
+import concourse.mybir as mybir
+from concourse.masks import make_identity
+
+F32 = mybir.dt.float32
+BF16 = mybir.dt.bfloat16
+U32 = mybir.dt.uint32
+U8 = mybir.dt.uint8
+FP8X4 = mybir.dt.float8_e4m3fn_x4
+ACT = mybir.ActivationFunctionType
+ALU = mybir.AluOpType
+AX = mybir.AxisListType
+
+P = 128
+ROWS = 4096
+K = 1024
+DOUT = 1024
+RT = ROWS // P
+KB = K // P
+MT = DOUT // P
+EPS = 1e-5
+FLOPS = 2 * ROWS * K * DOUT
+
+N_S = 2
+KB_V = KB - N_S
+N_ONES = 256
+S_REGROUP = {0: (1, 2, 3), 1: (1, 2, 3), 2: (1, 2, 3), 3: (1, 3)}
+STORE_GROUPS = ((0, 1), (2, 3), (4,), (5,), (6,), (7,))
+LAG = 3
+
+
+def tile_settransform_pa_t_kernel(tc, set_feats, g0, b0, W0, c0, g1, b1, out):
+    nc = tc.nc
+    x_v = set_feats.flatten_outer_dims().rearrange("(p j) k -> p j k", j=RT)
+    out_v = out.flatten_outer_dims().rearrange("(p j) d -> p j d", j=RT)
+    w_v = W0.rearrange("(m p) k -> p m k", p=P)
+
+    with ExitStack() as ctx:
+        const = ctx.enter_context(tc.tile_pool(name="const", bufs=1))
+        big = ctx.enter_context(tc.tile_pool(name="big", bufs=4))
+        small = ctx.enter_context(tc.tile_pool(name="small", bufs=3))
+
+        eps_t = const.tile([P, 1], F32, name="eps_t")
+        nc.vector.memset(eps_t[:], EPS)
+        warm = const.tile([P, 1], F32, name="warm")
+        nc.scalar.activation(out=warm[:], in_=eps_t[:], func=ACT.Sqrt)
+
+        ident_bf = const.tile([P, P], BF16, name="ident_bf")
+        make_identity(nc, ident_bf[:])
+        ident_f = const.tile([P, P], F32, name="ident_f")
+        make_identity(nc, ident_f[:])
+        ones_bf = const.tile([P, N_ONES], BF16, name="ones_bf")
+        nc.vector.memset(ones_bf[:], 1.0)
+        praw = const.tile([P, 512], BF16, name="praw")
+        nc.vector.memset(praw[:], 0.0)
+
+        par = const.tile([P, 40], F32, name="par")
+        gpair = const.tile([P, MT, 2], F32, name="gpair")
+        xq = [const.tile([P, 2, 1024], U32, name="xq%d" % q, align_bytes=64) for q in range(4)]
+        xsc = [const.tile([P, 2, 1024], U8, name="xsc%d" % q, align_bytes=64) for q in range(4)]
+        wq = const.tile([P, 2, DOUT], U32, name="wq", align_bytes=64)
+        wsc = const.tile([P, 2, DOUT], U8, name="wsc", align_bytes=64)
+        st0 = const.tile([P, KB_V, 8, 6], F32, name="st0")
+        mv0 = const.tile([P, KB, 2], F32, name="mv0")
+        nmu = const.tile([P, N_S], F32, name="nmu")
+        sq = const.tile([P, N_S, 8], F32, name="sq")
+
+        ctx.enter_context(tc.manual_schedule())
+
+        with ExitStack() as actx:
+            xpool = actx.enter_context(tc.tile_pool(name="xpool", bufs=4))
+            wpool = actx.enter_context(tc.tile_pool(name="wpool", bufs=1))
+            gpool = actx.enter_context(tc.tile_pool(name="gpool", bufs=3))
+            jpool = actx.enter_context(tc.tile_pool(name="jpool", bufs=2))
+            ps_a = actx.enter_context(tc.psum_pool(name="ps_a", bufs=6))
+            ps_s = actx.enter_context(tc.psum_pool(name="ps_s", bufs=1))
+
+            for i, v in enumerate((g0, b0, c0, g1, b1)):
+                nc.scalar.dma_start(out=praw[2 * i : 2 * i + 2, :], in_=v.rearrange("(g f) -> g f", g=2))
+
+            xT = [big.tile([P, KB, 1024], BF16, name="xT%d" % q, tag="big") for q in range(4)]
+            w_sb = wpool.tile([P, MT, K], BF16, name="w_sb")
+            wg = wpool.tile([P, 2, DOUT, 4], BF16, name="wg", align_bytes=64)
+            sums = [ps_s.tile([P, N_ONES], F32, name="sums%d" % i) for i in range(N_S)]
+            first = ps_a.tile([P, N_S, 32], F32, name="first", tag="tp")
+
+            def feats(kb):
+                g, t = kb // 4, kb % 4
+                return slice(512 * g + t, 512 * g + t + 4 * (P - 1) + 1, 4)
+
+            def w_tile(m):
+                for g in range(2):
+                    pt = ps_a.tile([P, 4, P], BF16, name="ptw", tag="tp")
+                    for t in range(4):
+                        kb = 4 * g + t
+                        nc.tensor.transpose(pt[:, t, :], w_sb[:, m, feats(kb)], ident_bf[:])
+                    nc.scalar.copy(out=wg[:, g, m * P : (m + 1) * P, :], in_=pt[:].rearrange("p t d -> p d t"))
+
+            for c in range(8):
+                x_sb = xpool.tile([P, 4, K], BF16, name="x_sb", tag="x_sb")
+                if c == 0:
+                    for hk in range(2):
+                        nc.sync.dma_start(
+                            out=x_sb[:, :, hk * 512 : (hk + 1) * 512], in_=x_v[:, 0:4, hk * 512 : (hk + 1) * 512]
+                        )
+                else:
+                    nc.sync.dma_start(out=x_sb[:], in_=x_v[:, 4 * c : 4 * c + 4, :])
+                if c == 3:
+                    nc.sync.dma_start(out=w_sb[:], in_=w_v)
+                base = (c % 2) * 512
+                if c == 0:
+                    for i in range(N_S):
+                        nc.tensor.matmul(
+                            out=first[:, i, :], lhsT=x_sb[:, 0, feats(i)], rhs=ones_bf[:, 0:32],
+                            start=True, stop=True,
+                        )
+                    nc.scalar.activation(out=nmu[:], in_=first[:, :, 0], func=ACT.Copy, scale=-1.0 / P)
+                for kb in range(KB):
+                    pt = ps_a.tile([P, 4, P], BF16, name="pt", tag="tp")
+                    for jj in range(4):
+                        nc.tensor.transpose(pt[:, jj, :], x_sb[:, jj, feats(kb)], ident_bf[:])
+                    i, jj = kb // 4, kb % 4
+                    nc.tensor.matmul(
+                        out=sums[i][:], lhsT=x_sb[:, jj, feats(i)], rhs=ones_bf[:],
+                        start=(c == 0 and jj == 0), stop=(c == 7 and jj == 3),
+                    )
+                    dst = xT[c // 2][:, kb, base : base + 512]
+                    src = pt[:].rearrange("p j r -> p (j r)")
+                    if kb == 2 or (kb == 3 and c % 2 == 1):
+                        nc.vector.tensor_copy(out=dst, in_=src)
+                    else:
+                        nc.scalar.copy(out=dst, in_=src)
+                    if kb >= N_S:
+                        nc.vector.bn_stats(out=st0[:, kb - N_S, c, :], in_=dst)
+                    if kb in (3, 6):
+                        i = kb // 3 - 1
+                        junk = jpool.tile([P, 512], BF16, name="junk", tag="junk")
+                        nc.scalar.activation(
+                            out=junk[:], in_=xT[c // 2][:, i, base : base + 512], func=ACT.Square,
+                            bias=nmu[:, i : i + 1], scale=1.0, accum_out=sq[:, i, c : c + 1],
+                        )
+                if 3 <= c <= 6:
+                    w_tile(c - 3)
+                if c == 2:
+                    pps = ps_a.tile([P, 4, P], BF16, name="pps", tag="tp")
+                    for t in range(4):
+                        nc.tensor.transpose(pps[:, t, :], praw[:, t : t + 4 * (P - 1) + 1 : 4], ident_bf[:])
+                    nc.vector.tensor_copy(
+                        out=par[:, 0:16].rearrange("p (r t) -> p r t", t=4),
+                        in_=pps[:, :, 0:4].rearrange("p t r -> p r t"),
+                    )
+                    ppo = ps_a.tile([P, 4, P], BF16, name="ppo", tag="tp")
+                    for j in range(4):
+                        nc.tensor.transpose(ppo[:, j, :], praw[:, j * P : (j + 1) * P], ident_bf[:])
+                    nc.vector.tensor_copy(
+                        out=par[:, 16:40].rearrange("p (r j) -> p r j", j=4),
+                        in_=ppo[:, :, 4:10].rearrange("p j r -> p r j"),
+                    )
+                    nc.vector.tensor_copy(out=gpair[:, :, 0], in_=par[:, 24:32])
+                    nc.vector.tensor_scalar(
+                        out=gpair[:, :, 1], in0=par[:, 24:32], scalar1=-1.0, scalar2=None, op0=ALU.mult
+                    )
+
+            for kb in range(N_S, KB):
+                nc.vector.bn_aggr(out=mv0[:, kb, :], in_=st0[:, kb - N_S, :, :].rearrange("p c s -> p (c s)"))
+            for i in range(N_S):
+                nc.vector.tensor_scalar(
+                    out=mv0[:, i, 0:1], in0=sums[i][:, 0:1], scalar1=1.0 / ROWS, scalar2=None, op0=ALU.mult
+                )
+            sqs = const.tile([P, N_S], F32, name="sqs")
+            nc.vector.tensor_reduce(out=sqs[:], in_=sq[:], axis=AX.X, op=ALU.add)
+            dl = const.tile([P, N_S], F32, name="dl")
+            nc.vector.tensor_tensor(out=dl[:], in0=mv0[:, 0:N_S, 0], in1=nmu[:], op=ALU.add)
+            dl2 = const.tile([P, N_S], F32, name="dl2")
+            nc.vector.tensor_tensor(out=dl2[:], in0=dl[:], in1=dl[:], op=ALU.mult)
+            nc.vector.scalar_tensor_tensor(
+                out=mv0[:, 0:N_S, 1], in0=sqs[:], scalar=1.0 / ROWS, in1=dl2[:], op0=ALU.mult, op1=ALU.subtract
+            )
+            w_tile(4)
+            w_tile(5)
+            sd0 = const.tile([P, KB], F32, name="sd0")
+            nc.scalar.activation(out=sd0[:], in_=mv0[:, :, 1], func=ACT.Sqrt, bias=eps_t[:, 0:1], scale=1.0)
+            w_tile(6)
+            w_tile(7)
+            r0 = const.tile([P, KB], F32, name="r0")
+            nc.vector.reciprocal(out=r0[:], in_=sd0[:])
+            a0 = const.tile([P, KB], F32, name="a0")
+            nc.vector.tensor_tensor(out=a0[:], in0=r0[:], in1=par[:, 0:8], op=ALU.mult)
+            ma0 = const.tile([P, KB], F32, name="ma0")
+            nc.vector.tensor_tensor(out=ma0[:], in0=mv0[:, :, 0], in1=a0[:], op=ALU.mult)
+            nd0 = const.tile([P, KB], F32, name="nd0")
+            nc.vector.tensor_tensor(out=nd0[:], in0=ma0[:], in1=par[:, 8:16], op=ALU.subtract)
+
+            def normalise_x(q):
+                for kb in range(KB):
+                    nc.vector.tensor_scalar(
+                        out=xT[q][:, kb, :], in0=xT[q][:, kb, :],
+                        scalar1=a0[:, kb : kb + 1], scalar2=nd0[:, kb : kb + 1],
+                        op0=ALU.mult, op1=ALU.subtract,
+                    )
+
+            normalise_x(0)
+            for q in range(4):
+                grs = []
+                for g in range(2):
+                    gr = gpool.tile([P, 1024, 4], BF16, name="gr", tag="gr", align_bytes=64)
+                    grs.append(gr)
+                    for hf in range(2):
+                        src = xT[q][:, 4 * g : 4 * g + 4, hf * 512 : (hf + 1) * 512]
+                        dst = gr[:, hf * 512 : (hf + 1) * 512, :]
+                        dst_v = dst.rearrange("p (c i) t -> p c t i", i=4)
+                        src_v = src.rearrange("p t (c i) -> p c t i", i=4)
+                        if 2 * g + hf in S_REGROUP[q]:
+                            nc.scalar.copy(out=dst_v, in_=src_v)
+                        else:
+                            nc.vector.tensor_copy(out=dst_v, in_=src_v)
+                if q + 1 < 4:
+                    normalise_x(q + 1)
+                if q == 0:
+                    for g in range(2):
+                        nc.vector.quantize_mx(
+                            out=wq[:, g, :].bitcast(FP8X4),
+                            scales=wsc[:, g, :],
+                            in_=wg[:, g, :, :].rearrange("p d t -> p (d t)"),
+                        )
+                for g in range(2):
+                    nc.vector.quantize_mx(
+                        out=xq[q][:, g, :].bitcast(FP8X4),
+                        scales=xsc[q][:, g, :],
+                        in_=grs[g][:].rearrange("p r t -> p (r t)"),
+                    )
+
+        with ExitStack() as bctx:
+            spool = bctx.enter_context(tc.tile_pool(name="spool", bufs=2))
+            ps_t = bctx.enter_context(tc.psum_pool(name="ps_t", bufs=4))
+            ps_m = bctx.enter_context(tc.psum_pool(name="ps_m", bufs=4))
+            h = {}
+            st1 = {}
+            stage = {}
+
+            def mx_burst(m, half):
+                if half == 0:
+                    h[m] = big.tile([P, ROWS], F32, name="h%d" % m, tag="big")
+                    st1[m] = small.tile([P, 8, 6], F32, name="st1", tag="st1")
+                accs = []
+                for c in range(4 * half, 4 * half + 4):
+                    acc = ps_m.tile([P, 512], F32, name="acc", tag="acc")
+                    accs.append(acc)
+                    q, hf = c // 2, c % 2
+                    for g in range(2):
+                        nc.tensor.matmul_mx(
+                            out=acc[:],
+                            lhsT=wq[:, g, m * P : (m + 1) * P].bitcast(FP8X4),
+                            lhsT_scale=wsc[:, g, m * P : (m + 1) * P],
+                            rhs=xq[q][:, g, hf * 512 : (hf + 1) * 512].bitcast(FP8X4),
+                            rhs_scale=xsc[q][:, g, hf * 512 : (hf + 1) * 512],
+                            start=(g == 0),
+                            stop=(g == 1),
+                        )
+                for n, acc in enumerate(accs):
+                    c = 4 * half + n
+                    nc.scalar.activation(
+                        out=h[m][:, c * 512 : (c + 1) * 512], in_=acc[:], func=ACT.Relu,
+                        bias=par[:, 16 + m : 17 + m], scale=1.0,
+                    )
+                    nc.vector.bn_stats(out=st1[m][:, c, :], in_=h[m][:, c * 512 : (c + 1) * 512])
+
+            def t_burst(m, half, spare):
+                banks = []
+                for c in range(4 * half, 4 * half + 4):
+                    if spare:
+                        pt = ps_m.tile([P, 4, P], F32, name="pts", tag="acc")
+                    else:
+                        pt = ps_t.tile([P, 4, P], F32, name="pto", tag="tp")
+                    banks.append(pt)
+                    for jj in range(4):
+                        j = 4 * c + jj
+                        nc.tensor.transpose(pt[:, jj, :], h[m][:, j * P : (j + 1) * P], ident_f[:])
+                return banks
+
+            def evac(m, c, pt, on_vector):
+                grp = [gr_ for gr_ in STORE_GROUPS if m in gr_][0]
+                gi = grp.index(m)
+                width = len(grp) * P
+                if gi == 0 and c == 0:
+                    stage[grp] = spool.tile([P, RT, width], F32, name="stage", tag="stage")
+                stg = stage[grp]
+                dst = stg[:, 4 * c : 4 * c + 4, gi * P : (gi + 1) * P]
+                if on_vector:
+                    nc.vector.tensor_copy(out=dst, in_=pt[:])
+                else:
+                    nc.scalar.copy(out=dst, in_=pt[:])
+                if gi == len(grp) - 1 and c % 2 == 1:
+                    s = c // 2
+                    nc.sync.dma_start(
+                        out=out_v[:, 8 * s : 8 * s + 8, grp[0] * P : grp[0] * P + width],
+                        in_=stg[:, 8 * s : 8 * s + 8, :],
+                    )
+
+            for step in range(2 * MT + LAG):
+                m, half = step // 2, step % 2
+                mt, th = (step - LAG) // 2, (step - LAG) % 2
+                close = m < MT and half == 1
+                if m < MT:
+                    mx_burst(m, half)
+                if close:
+                    mv = small.tile([P, 2], F32, name="mv", tag="mv")
+                    nc.vector.bn_aggr(out=mv[:], in_=st1[m][:].rearrange("p c s -> p (c s)"))
+                banks = t_burst(mt, th, step == 2 * MT + 1) if step >= LAG else []
+                if banks:
+                    evac(mt, 4 * th, banks[0], False)
+                    evac(mt, 4 * th + 1, banks[1], True)
+                if close:
+                    sd = small.tile([P, 1], F32, name="sd", tag="sd")
+                    nc.scalar.activation(out=sd[:], in_=mv[:, 1:2], func=ACT.Sqrt, bias=eps_t[:, 0:1], scale=1.0)
+                    r1 = small.tile([P, 1], F32, name="r1", tag="r1")
+                    nc.vector.reciprocal(out=r1[:], in_=sd[:])
+                    a1 = small.tile([P, 2], F32, name="a1", tag="a1")
+                    nc.vector.tensor_scalar(
+                        out=a1[:], in0=gpair[:, m, :], scalar1=r1[:, 0:1], scalar2=None, op0=ALU.mult
+                    )
+                    d1 = small.tile([P, 1], F32, name="d1", tag="d1")
+                    nc.vector.scalar_tensor_tensor(
+                        out=d1[:], in0=mv[:, 0:1], scalar=a1[:, 1:2], in1=par[:, 32 + m : 33 + m],
+                        op0=ALU.mult, op1=ALU.add,
+                    )
+                    for s in range(4):
+                        hs = h[m][:, s * 1024 : (s + 1) * 1024]
+                        if m == MT - 1 and s == 1:
+                            nc.scalar.activation(
+                                out=hs, in_=hs, func=ACT.Identity, bias=d1[:, 0:1], scale=a1[:, 0:1]
+                            )
+                        elif m == MT - 1 and s == 0:
+                            nc.vector.tensor_scalar(
+                                out=hs, in0=hs, scalar1=a1[:, 0:1], scalar2=d1[:, 0:1], op0=ALU.mult, op1=ALU.add
+                            )
+                        else:
+                            nc.gpsimd.tensor_scalar(
+                                out=hs, in0=hs, scalar1=a1[:, 0:1], scalar2=d1[:, 0:1], op0=ALU.mult, op1=ALU.add
+                            )
+                if banks:
+                    evac(mt, 4 * th + 2, banks[2], False)
+                    evac(mt, 4 * th + 3, banks[3], True)

@@ -19,15 +19,16 @@ DOUT = 1024
 RT = ROWS // P
 KB = K // P
 MT = DOUT // P
+CH = 512
+NCH = ROWS // CH
 EPS = 1e-5
 FLOPS = 2 * ROWS * K * DOUT
 
 N_S = 2
 KB_V = KB - N_S
 N_ONES = 256
-S_REGROUP = {0: (1, 2, 3), 1: (1, 2, 3), 2: (1, 2, 3), 3: (1, 3)}
-STORE_GROUPS = ((0, 1), (2, 3), (4,), (5,), (6,), (7,))
-LAG = 3
+STORE_GROUPS = ((0, 1), (2, 3), (4, 5), (6,), (7,))
+LAG = 1
 
 
 def tile_settransform_pa_t_kernel(tc, set_feats, g0, b0, W0, c0, g1, b1, out):
@@ -57,288 +58,305 @@ def tile_settransform_pa_t_kernel(tc, set_feats, g0, b0, W0, c0, g1, b1, out):
 
         par = const.tile([P, 40], F32, name="par")
         gpair = const.tile([P, MT, 2], F32, name="gpair")
-        xq = [const.tile([P, 2, 1024], U32, name="xq%d" % q, align_bytes=64) for q in range(4)]
-        xsc = [const.tile([P, 2, 1024], U8, name="xsc%d" % q, align_bytes=64) for q in range(4)]
+        xq = [const.tile([P, 2 * CH], U32, name="xq%d" % c, align_bytes=64) for c in range(NCH)]
+        xsc = [const.tile([P, 2 * CH], U8, name="xsc%d" % c, align_bytes=64) for c in range(NCH)]
         wq = const.tile([P, 2, DOUT], U32, name="wq", align_bytes=64)
         wsc = const.tile([P, 2, DOUT], U8, name="wsc", align_bytes=64)
         st0 = const.tile([P, KB_V, 8, 6], F32, name="st0")
         mv0 = const.tile([P, KB, 2], F32, name="mv0")
         nmu = const.tile([P, N_S], F32, name="nmu")
         sq = const.tile([P, N_S, 8], F32, name="sq")
+        st1 = [const.tile([P, NCH, 6], F32, name="st1_%d" % m) for m in range(MT)]
+        h = {}
 
         ctx.enter_context(tc.manual_schedule())
 
+        def h_tile(q, mh):
+            tag = "hx" if mh == 0 else "ht"
+            h[q, mh] = big.tile([P, 8, 4, P], F32, name="h%d_%d" % (q, mh), tag=tag, align_bytes=64)
+
+        def h_part(m, c):
+            return h[c // 2, m // 4][:, 4 * (c % 2) : 4 * (c % 2) + 4, m % 4, :]
+
+        def mx(pool, m, c):
+            if (c // 2, m // 4) not in h:
+                h_tile(c // 2, m // 4)
+            acc = pool.tile([P, 4, P], F32, name="acc", tag="acc")
+            for g in range(2):
+                nc.tensor.matmul_mx(
+                    out=acc[:].rearrange("p j r -> p (j r)"),
+                    lhsT=wq[:, g, m * P : (m + 1) * P].bitcast(FP8X4),
+                    lhsT_scale=wsc[:, g, m * P : (m + 1) * P],
+                    rhs=xq[c][:, g * CH : (g + 1) * CH].bitcast(FP8X4),
+                    rhs_scale=xsc[c][:, g * CH : (g + 1) * CH],
+                    start=(g == 0),
+                    stop=(g == 1),
+                )
+            return acc
+
+        def relu(m, c, acc):
+            nc.scalar.activation(
+                out=h_part(m, c), in_=acc[:], func=ACT.Relu, bias=par[:, 16 + m : 17 + m], scale=1.0
+            )
+
+        def bn(m, c):
+            nc.vector.bn_stats(out=st1[m][:, c, :], in_=h_part(m, c))
+
         with ExitStack() as actx:
-            xpool = actx.enter_context(tc.tile_pool(name="xpool", bufs=4))
             wpool = actx.enter_context(tc.tile_pool(name="wpool", bufs=1))
-            gpool = actx.enter_context(tc.tile_pool(name="gpool", bufs=3))
+            gpool = actx.enter_context(tc.tile_pool(name="gpool", bufs=4))
             jpool = actx.enter_context(tc.tile_pool(name="jpool", bufs=2))
-            ps_a = actx.enter_context(tc.psum_pool(name="ps_a", bufs=6))
-            ps_s = actx.enter_context(tc.psum_pool(name="ps_s", bufs=1))
 
             for i, v in enumerate((g0, b0, c0, g1, b1)):
                 nc.scalar.dma_start(out=praw[2 * i : 2 * i + 2, :], in_=v.rearrange("(g f) -> g f", g=2))
 
-            xT = [big.tile([P, KB, 1024], BF16, name="xT%d" % q, tag="big") for q in range(4)]
+            xs = [big.tile([P, 8, K], BF16, name="xs%d" % q, tag="hx", align_bytes=64) for q in range(4)]
+            xT = [big.tile([P, KB, 1024], BF16, name="xT%d" % q, tag="ht", align_bytes=64) for q in range(4)]
             w_sb = wpool.tile([P, MT, K], BF16, name="w_sb")
-            wg = wpool.tile([P, 2, DOUT, 4], BF16, name="wg", align_bytes=64)
-            sums = [ps_s.tile([P, N_ONES], F32, name="sums%d" % i) for i in range(N_S)]
-            first = ps_a.tile([P, N_S, 32], F32, name="first", tag="tp")
+            wg = [gpool.tile([P, 4 * DOUT], BF16, name="wg%d" % g, tag="gr", align_bytes=64) for g in range(2)]
 
-            def feats(kb):
-                g, t = kb // 4, kb % 4
-                return slice(512 * g + t, 512 * g + t + 4 * (P - 1) + 1, 4)
+            with ExitStack() as pctx:
+                ps_a = pctx.enter_context(tc.psum_pool(name="ps_a", bufs=6))
+                ps_s = pctx.enter_context(tc.psum_pool(name="ps_s", bufs=1))
+                sums = [ps_s.tile([P, N_ONES], F32, name="sums%d" % i) for i in range(N_S)]
+                first = ps_a.tile([P, N_S, 32], F32, name="first", tag="tp")
 
-            def w_tile(m):
-                for g in range(2):
-                    pt = ps_a.tile([P, 4, P], BF16, name="ptw", tag="tp")
-                    for t in range(4):
-                        kb = 4 * g + t
-                        nc.tensor.transpose(pt[:, t, :], w_sb[:, m, feats(kb)], ident_bf[:])
-                    nc.scalar.copy(out=wg[:, g, m * P : (m + 1) * P, :], in_=pt[:].rearrange("p t d -> p d t"))
+                def feats(kb):
+                    g, t = kb // 4, kb % 4
+                    return slice(512 * g + t, 512 * g + t + 4 * (P - 1) + 1, 4)
 
-            for c in range(8):
-                x_sb = xpool.tile([P, 4, K], BF16, name="x_sb", tag="x_sb")
-                if c == 0:
-                    for hk in range(2):
-                        nc.sync.dma_start(
-                            out=x_sb[:, :, hk * 512 : (hk + 1) * 512], in_=x_v[:, 0:4, hk * 512 : (hk + 1) * 512]
+                def w_tile(m):
+                    words = w_sb[:, m, :].bitcast(F32)
+                    pt = ps_a.tile([P, 2, 2, P], F32, name="ptw", tag="tp")
+                    for g in range(2):
+                        for u in range(2):
+                            lo = 256 * g + u
+                            nc.tensor.transpose(pt[:, g, u, :], words[:, lo : lo + 2 * (P - 1) + 1 : 2], ident_f[:])
+                    for g in range(2):
+                        nc.scalar.copy(
+                            out=wg[g][:, 4 * m * P : 4 * (m + 1) * P].bitcast(F32).rearrange("p (d u) -> p d u", u=2),
+                            in_=pt[:, g, :, :].rearrange("p u d -> p d u"),
                         )
-                else:
-                    nc.sync.dma_start(out=x_sb[:], in_=x_v[:, 4 * c : 4 * c + 4, :])
-                if c == 3:
-                    nc.sync.dma_start(out=w_sb[:], in_=w_v)
-                base = (c % 2) * 512
-                if c == 0:
-                    for i in range(N_S):
-                        nc.tensor.matmul(
-                            out=first[:, i, :], lhsT=x_sb[:, 0, feats(i)], rhs=ones_bf[:, 0:32],
-                            start=True, stop=True,
-                        )
-                    nc.scalar.activation(out=nmu[:], in_=first[:, :, 0], func=ACT.Copy, scale=-1.0 / P)
-                for kb in range(KB):
-                    pt = ps_a.tile([P, 4, P], BF16, name="pt", tag="tp")
-                    for jj in range(4):
-                        nc.tensor.transpose(pt[:, jj, :], x_sb[:, jj, feats(kb)], ident_bf[:])
-                    i, jj = kb // 4, kb % 4
-                    nc.tensor.matmul(
-                        out=sums[i][:], lhsT=x_sb[:, jj, feats(i)], rhs=ones_bf[:],
-                        start=(c == 0 and jj == 0), stop=(c == 7 and jj == 3),
-                    )
-                    dst = xT[c // 2][:, kb, base : base + 512]
-                    src = pt[:].rearrange("p j r -> p (j r)")
-                    if kb == 2 or (kb == 3 and c % 2 == 1):
-                        nc.vector.tensor_copy(out=dst, in_=src)
+
+                for c in range(NCH):
+                    j0 = 4 * (c % 2)
+                    x_sb = xs[c // 2][:, j0 : j0 + 4, :]
+                    if c == 0:
+                        for hk in range(2):
+                            nc.sync.dma_start(
+                                out=x_sb[:, :, hk * 512 : (hk + 1) * 512], in_=x_v[:, 0:4, hk * 512 : (hk + 1) * 512]
+                            )
                     else:
-                        nc.scalar.copy(out=dst, in_=src)
-                    if kb >= N_S:
-                        nc.vector.bn_stats(out=st0[:, kb - N_S, c, :], in_=dst)
-                    if kb in (3, 6):
-                        i = kb // 3 - 1
-                        junk = jpool.tile([P, 512], BF16, name="junk", tag="junk")
-                        nc.scalar.activation(
-                            out=junk[:], in_=xT[c // 2][:, i, base : base + 512], func=ACT.Square,
-                            bias=nmu[:, i : i + 1], scale=1.0, accum_out=sq[:, i, c : c + 1],
+                        nc.sync.dma_start(out=x_sb, in_=x_v[:, 4 * c : 4 * c + 4, :])
+                    if c == 3:
+                        nc.sync.dma_start(out=w_sb[:], in_=w_v)
+                    base = (c % 2) * CH
+                    if c == 0:
+                        for i in range(N_S):
+                            nc.tensor.matmul(
+                                out=first[:, i, :], lhsT=x_sb[:, 0, feats(i)], rhs=ones_bf[:, 0:32],
+                                start=True, stop=True,
+                            )
+                        nc.scalar.activation(out=nmu[:], in_=first[:, :, 0], func=ACT.Copy, scale=-1.0 / P)
+                    for kb in range(KB):
+                        pt = ps_a.tile([P, 4, P], BF16, name="pt", tag="tp")
+                        for jj in range(4):
+                            nc.tensor.transpose(pt[:, jj, :], x_sb[:, jj, feats(kb)], ident_bf[:])
+                        i, jj = kb // 4, kb % 4
+                        nc.tensor.matmul(
+                            out=sums[i][:], lhsT=x_sb[:, jj, feats(i)], rhs=ones_bf[:],
+                            start=(c == 0 and jj == 0), stop=(c == 7 and jj == 3),
                         )
-                if 3 <= c <= 6:
-                    w_tile(c - 3)
-                if c == 2:
-                    pps = ps_a.tile([P, 4, P], BF16, name="pps", tag="tp")
-                    for t in range(4):
-                        nc.tensor.transpose(pps[:, t, :], praw[:, t : t + 4 * (P - 1) + 1 : 4], ident_bf[:])
-                    nc.vector.tensor_copy(
-                        out=par[:, 0:16].rearrange("p (r t) -> p r t", t=4),
-                        in_=pps[:, :, 0:4].rearrange("p t r -> p r t"),
-                    )
-                    ppo = ps_a.tile([P, 4, P], BF16, name="ppo", tag="tp")
-                    for j in range(4):
-                        nc.tensor.transpose(ppo[:, j, :], praw[:, j * P : (j + 1) * P], ident_bf[:])
-                    nc.vector.tensor_copy(
-                        out=par[:, 16:40].rearrange("p (r j) -> p r j", j=4),
-                        in_=ppo[:, :, 4:10].rearrange("p j r -> p r j"),
-                    )
-                    nc.vector.tensor_copy(out=gpair[:, :, 0], in_=par[:, 24:32])
-                    nc.vector.tensor_scalar(
-                        out=gpair[:, :, 1], in0=par[:, 24:32], scalar1=-1.0, scalar2=None, op0=ALU.mult
-                    )
+                        dst = xT[c // 2][:, kb, base : base + CH]
+                        nc.scalar.copy(out=dst, in_=pt[:].rearrange("p j r -> p (j r)"))
+                        if kb >= N_S:
+                            nc.vector.bn_stats(out=st0[:, kb - N_S, c, :], in_=dst)
+                        if kb in (3, 6):
+                            i = kb // 3 - 1
+                            junk = jpool.tile([P, CH], BF16, name="junk", tag="junk")
+                            nc.scalar.activation(
+                                out=junk[:], in_=xT[c // 2][:, i, base : base + CH], func=ACT.Square,
+                                bias=nmu[:, i : i + 1], scale=1.0, accum_out=sq[:, i, c : c + 1],
+                            )
+                    if c == 2:
+                        pps = ps_a.tile([P, 4, P], BF16, name="pps", tag="tp")
+                        for t in range(4):
+                            nc.tensor.transpose(pps[:, t, :], praw[:, t : t + 4 * (P - 1) + 1 : 4], ident_bf[:])
+                        nc.vector.tensor_copy(
+                            out=par[:, 0:16].rearrange("p (r t) -> p r t", t=4),
+                            in_=pps[:, :, 0:4].rearrange("p t r -> p r t"),
+                        )
+                        ppo = ps_a.tile([P, 4, P], BF16, name="ppo", tag="tp")
+                        for j in range(4):
+                            nc.tensor.transpose(ppo[:, j, :], praw[:, j * P : (j + 1) * P], ident_bf[:])
+                        nc.vector.tensor_copy(
+                            out=par[:, 16:40].rearrange("p (r j) -> p r j", j=4),
+                            in_=ppo[:, :, 4:10].rearrange("p j r -> p r j"),
+                        )
+                        nc.vector.tensor_copy(out=gpair[:, :, 0], in_=par[:, 24:32])
+                        nc.vector.tensor_scalar(
+                            out=gpair[:, :, 1], in0=par[:, 24:32], scalar1=-1.0, scalar2=None, op0=ALU.mult
+                        )
 
-            for kb in range(N_S, KB):
-                nc.vector.bn_aggr(out=mv0[:, kb, :], in_=st0[:, kb - N_S, :, :].rearrange("p c s -> p (c s)"))
-            for i in range(N_S):
-                nc.vector.tensor_scalar(
-                    out=mv0[:, i, 0:1], in0=sums[i][:, 0:1], scalar1=1.0 / ROWS, scalar2=None, op0=ALU.mult
+                w_tile(0)
+                for kb in range(N_S, KB):
+                    nc.vector.bn_aggr(out=mv0[:, kb, :], in_=st0[:, kb - N_S, :, :].rearrange("p c s -> p (c s)"))
+                for i in range(N_S):
+                    nc.vector.tensor_scalar(
+                        out=mv0[:, i, 0:1], in0=sums[i][:, 0:1], scalar1=1.0 / ROWS, scalar2=None, op0=ALU.mult
+                    )
+                sqs = const.tile([P, N_S], F32, name="sqs")
+                nc.vector.tensor_reduce(out=sqs[:], in_=sq[:], axis=AX.X, op=ALU.add)
+                dl = const.tile([P, N_S], F32, name="dl")
+                nc.vector.tensor_tensor(out=dl[:], in0=mv0[:, 0:N_S, 0], in1=nmu[:], op=ALU.add)
+                dl2 = const.tile([P, N_S], F32, name="dl2")
+                nc.vector.tensor_tensor(out=dl2[:], in0=dl[:], in1=dl[:], op=ALU.mult)
+                nc.vector.scalar_tensor_tensor(
+                    out=mv0[:, 0:N_S, 1], in0=sqs[:], scalar=1.0 / ROWS, in1=dl2[:], op0=ALU.mult, op1=ALU.subtract
                 )
-            sqs = const.tile([P, N_S], F32, name="sqs")
-            nc.vector.tensor_reduce(out=sqs[:], in_=sq[:], axis=AX.X, op=ALU.add)
-            dl = const.tile([P, N_S], F32, name="dl")
-            nc.vector.tensor_tensor(out=dl[:], in0=mv0[:, 0:N_S, 0], in1=nmu[:], op=ALU.add)
-            dl2 = const.tile([P, N_S], F32, name="dl2")
-            nc.vector.tensor_tensor(out=dl2[:], in0=dl[:], in1=dl[:], op=ALU.mult)
-            nc.vector.scalar_tensor_tensor(
-                out=mv0[:, 0:N_S, 1], in0=sqs[:], scalar=1.0 / ROWS, in1=dl2[:], op0=ALU.mult, op1=ALU.subtract
-            )
-            w_tile(4)
-            w_tile(5)
-            sd0 = const.tile([P, KB], F32, name="sd0")
-            nc.scalar.activation(out=sd0[:], in_=mv0[:, :, 1], func=ACT.Sqrt, bias=eps_t[:, 0:1], scale=1.0)
-            w_tile(6)
-            w_tile(7)
-            r0 = const.tile([P, KB], F32, name="r0")
-            nc.vector.reciprocal(out=r0[:], in_=sd0[:])
-            a0 = const.tile([P, KB], F32, name="a0")
-            nc.vector.tensor_tensor(out=a0[:], in0=r0[:], in1=par[:, 0:8], op=ALU.mult)
-            ma0 = const.tile([P, KB], F32, name="ma0")
-            nc.vector.tensor_tensor(out=ma0[:], in0=mv0[:, :, 0], in1=a0[:], op=ALU.mult)
-            nd0 = const.tile([P, KB], F32, name="nd0")
-            nc.vector.tensor_tensor(out=nd0[:], in0=ma0[:], in1=par[:, 8:16], op=ALU.subtract)
+                w_tile(1)
+                w_tile(2)
+                sd0 = const.tile([P, KB], F32, name="sd0")
+                nc.scalar.activation(out=sd0[:], in_=mv0[:, :, 1], func=ACT.Sqrt, bias=eps_t[:, 0:1], scale=1.0)
+                for m in range(3, MT):
+                    w_tile(m)
+                r0 = const.tile([P, KB], F32, name="r0")
+                nc.vector.reciprocal(out=r0[:], in_=sd0[:])
+                a0 = const.tile([P, KB], F32, name="a0")
+                nc.vector.tensor_tensor(out=a0[:], in0=r0[:], in1=par[:, 0:8], op=ALU.mult)
+                ma0 = const.tile([P, KB], F32, name="ma0")
+                nc.vector.tensor_tensor(out=ma0[:], in0=mv0[:, :, 0], in1=a0[:], op=ALU.mult)
+                nd0 = const.tile([P, KB], F32, name="nd0")
+                nc.vector.tensor_tensor(out=nd0[:], in0=ma0[:], in1=par[:, 8:16], op=ALU.subtract)
 
-            def normalise_x(q):
+            ps_t = ctx.enter_context(tc.psum_pool(name="ps_t", bufs=4))
+            ps_m = ctx.enter_context(tc.psum_pool(name="ps_m", bufs=4))
+            gr = {}
+
+            def normalise_x(c):
+                base = (c % 2) * CH
                 for kb in range(KB):
+                    xs_ = xT[c // 2][:, kb, base : base + CH]
                     nc.vector.tensor_scalar(
-                        out=xT[q][:, kb, :], in0=xT[q][:, kb, :],
-                        scalar1=a0[:, kb : kb + 1], scalar2=nd0[:, kb : kb + 1],
+                        out=xs_, in0=xs_, scalar1=a0[:, kb : kb + 1], scalar2=nd0[:, kb : kb + 1],
                         op0=ALU.mult, op1=ALU.subtract,
                     )
 
-            normalise_x(0)
-            for q in range(4):
-                grs = []
-                for g in range(2):
-                    gr = gpool.tile([P, 1024, 4], BF16, name="gr", tag="gr", align_bytes=64)
-                    grs.append(gr)
-                    for hf in range(2):
-                        src = xT[q][:, 4 * g : 4 * g + 4, hf * 512 : (hf + 1) * 512]
-                        dst = gr[:, hf * 512 : (hf + 1) * 512, :]
-                        dst_v = dst.rearrange("p (c i) t -> p c t i", i=4)
-                        src_v = src.rearrange("p t (c i) -> p c t i", i=4)
-                        if 2 * g + hf in S_REGROUP[q]:
-                            nc.scalar.copy(out=dst_v, in_=src_v)
-                        else:
-                            nc.vector.tensor_copy(out=dst_v, in_=src_v)
-                if q + 1 < 4:
-                    normalise_x(q + 1)
-                if q == 0:
-                    for g in range(2):
-                        nc.vector.quantize_mx(
-                            out=wq[:, g, :].bitcast(FP8X4),
-                            scales=wsc[:, g, :],
-                            in_=wg[:, g, :, :].rearrange("p d t -> p (d t)"),
-                        )
-                for g in range(2):
-                    nc.vector.quantize_mx(
-                        out=xq[q][:, g, :].bitcast(FP8X4),
-                        scales=xsc[q][:, g, :],
-                        in_=grs[g][:].rearrange("p r t -> p (r t)"),
-                    )
-
-        with ExitStack() as bctx:
-            spool = bctx.enter_context(tc.tile_pool(name="spool", bufs=2))
-            ps_t = bctx.enter_context(tc.psum_pool(name="ps_t", bufs=4))
-            ps_m = bctx.enter_context(tc.psum_pool(name="ps_m", bufs=4))
-            h = {}
-            st1 = {}
-            stage = {}
-
-            def mx_burst(m, half):
-                if half == 0:
-                    h[m] = big.tile([P, ROWS], F32, name="h%d" % m, tag="big")
-                    st1[m] = small.tile([P, 8, 6], F32, name="st1", tag="st1")
-                accs = []
-                for c in range(4 * half, 4 * half + 4):
-                    acc = ps_m.tile([P, 512], F32, name="acc", tag="acc")
-                    accs.append(acc)
-                    q, hf = c // 2, c % 2
-                    for g in range(2):
-                        nc.tensor.matmul_mx(
-                            out=acc[:],
-                            lhsT=wq[:, g, m * P : (m + 1) * P].bitcast(FP8X4),
-                            lhsT_scale=wsc[:, g, m * P : (m + 1) * P],
-                            rhs=xq[q][:, g, hf * 512 : (hf + 1) * 512].bitcast(FP8X4),
-                            rhs_scale=xsc[q][:, g, hf * 512 : (hf + 1) * 512],
-                            start=(g == 0),
-                            stop=(g == 1),
-                        )
-                for n, acc in enumerate(accs):
-                    c = 4 * half + n
-                    nc.scalar.activation(
-                        out=h[m][:, c * 512 : (c + 1) * 512], in_=acc[:], func=ACT.Relu,
-                        bias=par[:, 16 + m : 17 + m], scale=1.0,
-                    )
-                    nc.vector.bn_stats(out=st1[m][:, c, :], in_=h[m][:, c * 512 : (c + 1) * 512])
-
-            def t_burst(m, half, spare):
-                banks = []
-                for c in range(4 * half, 4 * half + 4):
-                    if spare:
-                        pt = ps_m.tile([P, 4, P], F32, name="pts", tag="acc")
-                    else:
-                        pt = ps_t.tile([P, 4, P], F32, name="pto", tag="tp")
-                    banks.append(pt)
-                    for jj in range(4):
-                        j = 4 * c + jj
-                        nc.tensor.transpose(pt[:, jj, :], h[m][:, j * P : (j + 1) * P], ident_f[:])
-                return banks
-
-            def evac(m, c, pt, on_vector):
-                grp = [gr_ for gr_ in STORE_GROUPS if m in gr_][0]
-                gi = grp.index(m)
-                width = len(grp) * P
-                if gi == 0 and c == 0:
-                    stage[grp] = spool.tile([P, RT, width], F32, name="stage", tag="stage")
-                stg = stage[grp]
-                dst = stg[:, 4 * c : 4 * c + 4, gi * P : (gi + 1) * P]
-                if on_vector:
-                    nc.vector.tensor_copy(out=dst, in_=pt[:])
+            def regroup(c, g, lo, hi, on_scalar):
+                base = (c % 2) * CH
+                src = xT[c // 2][:, 4 * g : 4 * g + 4, base + lo : base + hi].rearrange("p t (c i) -> p c t i", i=4)
+                dst = gr[c][:, 4 * (g * CH + lo) : 4 * (g * CH + hi)].rearrange("p (c i t) -> p c t i", i=4, t=4)
+                if on_scalar:
+                    nc.scalar.copy(out=dst, in_=src)
                 else:
-                    nc.scalar.copy(out=dst, in_=pt[:])
-                if gi == len(grp) - 1 and c % 2 == 1:
-                    s = c // 2
-                    nc.sync.dma_start(
-                        out=out_v[:, 8 * s : 8 * s + 8, grp[0] * P : grp[0] * P + width],
-                        in_=stg[:, 8 * s : 8 * s + 8, :],
+                    nc.vector.tensor_copy(out=dst, in_=src)
+
+            def quantise_x(c):
+                nc.vector.quantize_mx(out=xq[c][:].bitcast(FP8X4), scales=xsc[c][:], in_=gr[c][:])
+
+            for i in range(NCH + 1):
+                if i < NCH:
+                    gr[i] = gpool.tile([P, 8 * CH], BF16, name="gr", tag="gr", align_bytes=64)
+                    normalise_x(i)
+                if i == 1:
+                    for g in range(2):
+                        nc.vector.quantize_mx(out=wq[:, g, :].bitcast(FP8X4), scales=wsc[:, g, :], in_=wg[g][:])
+                if 1 <= i <= NCH:
+                    quantise_x(i - 1)
+                if i < NCH:
+                    cut = CH if i == 0 else (0 if i == 1 else 3 * CH // 4)
+                    regroup(i, 0, 0, CH, False)
+                    if cut > 0:
+                        regroup(i, 1, 0, cut, False)
+                    if cut < CH:
+                        regroup(i, 1, cut, CH, True)
+                if 1 <= i <= NCH:
+                    for m in range(MT):
+                        relu(m, i - 1, mx(ps_m, m, i - 1))
+                if 2 <= i <= NCH:
+                    bn(0, i - 2)
+            for c in range(4):
+                bn(1, c)
+            bn(0, NCH - 1)
+
+        stats = {}
+
+        def close_stats(m):
+            mv = small.tile([P, 2], F32, name="mv", tag="mv")
+            nc.vector.bn_aggr(out=mv[:], in_=st1[m][:].rearrange("p c s -> p (c s)"))
+            stats[m] = mv
+
+        def deviation(m):
+            mv = stats[m]
+            sd = small.tile([P, 1], F32, name="sd", tag="sd")
+            nc.scalar.activation(out=sd[:], in_=mv[:, 1:2], func=ACT.Sqrt, bias=eps_t[:, 0:1], scale=1.0)
+            stats[m] = (mv, sd)
+
+        def norm_out(m):
+            mv, sd = stats[m]
+            r1 = small.tile([P, 1], F32, name="r1", tag="r1")
+            nc.vector.reciprocal(out=r1[:], in_=sd[:])
+            a1 = small.tile([P, 2], F32, name="a1", tag="a1")
+            nc.vector.tensor_scalar(out=a1[:], in0=gpair[:, m, :], scalar1=r1[:, 0:1], scalar2=None, op0=ALU.mult)
+            d1 = small.tile([P, 1], F32, name="d1", tag="d1")
+            nc.vector.scalar_tensor_tensor(
+                out=d1[:], in0=mv[:, 0:1], scalar=a1[:, 1:2], in1=par[:, 32 + m : 33 + m], op0=ALU.mult, op1=ALU.add
+            )
+            engines = "VVSV" if m == MT - 1 else "VGGG"
+            for q in range(4):
+                hs = h[q, m // 4][:, :, m % 4, :]
+                if engines[q] == "S":
+                    nc.scalar.activation(out=hs, in_=hs, func=ACT.Identity, bias=d1[:, 0:1], scale=a1[:, 0:1])
+                else:
+                    eng = nc.vector if engines[q] == "V" else nc.gpsimd
+                    eng.tensor_scalar(
+                        out=hs, in0=hs, scalar1=a1[:, 0:1], scalar2=d1[:, 0:1], op0=ALU.mult, op1=ALU.add
                     )
 
-            for step in range(2 * MT + LAG):
-                m, half = step // 2, step % 2
-                mt, th = (step - LAG) // 2, (step - LAG) % 2
-                close = m < MT and half == 1
-                if m < MT:
-                    mx_burst(m, half)
-                if close:
-                    mv = small.tile([P, 2], F32, name="mv", tag="mv")
-                    nc.vector.bn_aggr(out=mv[:], in_=st1[m][:].rearrange("p c s -> p (c s)"))
-                banks = t_burst(mt, th, step == 2 * MT + 1) if step >= LAG else []
-                if banks:
-                    evac(mt, 4 * th, banks[0], False)
-                    evac(mt, 4 * th + 1, banks[1], True)
-                if close:
-                    sd = small.tile([P, 1], F32, name="sd", tag="sd")
-                    nc.scalar.activation(out=sd[:], in_=mv[:, 1:2], func=ACT.Sqrt, bias=eps_t[:, 0:1], scale=1.0)
-                    r1 = small.tile([P, 1], F32, name="r1", tag="r1")
-                    nc.vector.reciprocal(out=r1[:], in_=sd[:])
-                    a1 = small.tile([P, 2], F32, name="a1", tag="a1")
-                    nc.vector.tensor_scalar(
-                        out=a1[:], in0=gpair[:, m, :], scalar1=r1[:, 0:1], scalar2=None, op0=ALU.mult
-                    )
-                    d1 = small.tile([P, 1], F32, name="d1", tag="d1")
-                    nc.vector.scalar_tensor_tensor(
-                        out=d1[:], in0=mv[:, 0:1], scalar=a1[:, 1:2], in1=par[:, 32 + m : 33 + m],
-                        op0=ALU.mult, op1=ALU.add,
-                    )
-                    for s in range(4):
-                        hs = h[m][:, s * 1024 : (s + 1) * 1024]
-                        if m == MT - 1 and s == 1:
-                            nc.scalar.activation(
-                                out=hs, in_=hs, func=ACT.Identity, bias=d1[:, 0:1], scale=a1[:, 0:1]
-                            )
-                        elif m == MT - 1 and s == 0:
-                            nc.vector.tensor_scalar(
-                                out=hs, in0=hs, scalar1=a1[:, 0:1], scalar2=d1[:, 0:1], op0=ALU.mult, op1=ALU.add
-                            )
-                        else:
-                            nc.gpsimd.tensor_scalar(
-                                out=hs, in0=hs, scalar1=a1[:, 0:1], scalar2=d1[:, 0:1], op0=ALU.mult, op1=ALU.add
-                            )
-                if banks:
-                    evac(mt, 4 * th + 2, banks[2], False)
-                    evac(mt, 4 * th + 3, banks[3], True)
+        def t_burst(m, half):
+            banks = []
+            for c in range(4 * half, 4 * half + 4):
+                pt = ps_t.tile([P, 4, P], F32, name="pto", tag="tp")
+                banks.append(pt)
+                for jj in range(4):
+                    nc.tensor.transpose(pt[:, jj, :], h_part(m, c)[:, jj, :], ident_f[:])
+            return banks
+
+        def evac(m, c, pt, on_vector):
+            if on_vector:
+                nc.vector.tensor_copy(out=h_part(m, c), in_=pt[:])
+            else:
+                nc.scalar.copy(out=h_part(m, c), in_=pt[:])
+            grp = [gr_ for gr_ in STORE_GROUPS if m in gr_][0]
+            if m == grp[-1] and c % 2 == 1:
+                q = c // 2
+                nc.sync.dma_start(
+                    out=out_v[:, 8 * q : 8 * q + 8, grp[0] * P : (m + 1) * P],
+                    in_=h[q, m // 4][:, :, grp[0] % 4 : m % 4 + 1, :].rearrange("p j m f -> p j (m f)"),
+                )
+
+        close_stats(0)
+        deviation(0)
+        for k in range(2 * MT + LAG):
+            mb, hb = 1 + k // 2, k % 2
+            chunks = range(4 * hb, 4 * hb + 4) if mb < MT and k > 0 else ()
+            tail = mb >= MT
+            banks = []
+            if hb == 0 and 0 < k and mb <= MT:
+                deviation(mb - 1)
+            if k >= LAG:
+                mt, th = (k - LAG) // 2, (k - LAG) % 2
+                banks = t_burst(mt, th)
+                evac(mt, 4 * th, banks[0], False)
+                evac(mt, 4 * th + 1, banks[1], tail)
+            for c in chunks[:2]:
+                bn(mb, c)
+            if hb == 0 and mb <= MT:
+                norm_out(mb - 1)
+            for c in chunks[2:]:
+                bn(mb, c)
+            if chunks and hb == 1:
+                close_stats(mb)
+            if banks:
+                evac(mt, 4 * th + 2, banks[2], False)
+                evac(mt, 4 * th + 3, banks[3], tail)

@@ -10,7 +10,6 @@ U8 = mybir.dt.uint8
 FP8X4 = mybir.dt.float8_e4m3fn_x4
 ACT = mybir.ActivationFunctionType
 ALU = mybir.AluOpType
-AX = mybir.AxisListType
 
 P = 128
 ROWS = 4096
@@ -24,9 +23,9 @@ NCH = ROWS // CH
 EPS = 1e-5
 FLOPS = 2 * ROWS * K * DOUT
 
-N_S = 2
-KB_V = KB - N_S
-N_ONES = 256
+PAD = 8
+NG = P + 2
+NM2 = 5
 STORE_GROUPS = ((0, 1), (2, 3), (4, 5), (6,), (7,))
 LAG = 1
 
@@ -40,53 +39,192 @@ def tile_settransform_pa_t_kernel(tc, set_feats, g0, b0, W0, c0, g1, b1, out):
     with ExitStack() as ctx:
         const = ctx.enter_context(tc.tile_pool(name="const", bufs=1))
         big = ctx.enter_context(tc.tile_pool(name="big", bufs=4))
+        gpool = ctx.enter_context(tc.tile_pool(name="gpool", bufs=3))
         small = ctx.enter_context(tc.tile_pool(name="small", bufs=3))
+        ps_t = ctx.enter_context(tc.psum_pool(name="ps_t", bufs=4))
 
         eps_t = const.tile([P, 1], F32, name="eps_t")
         nc.vector.memset(eps_t[:], EPS)
         warm = const.tile([P, 1], F32, name="warm")
         nc.scalar.activation(out=warm[:], in_=eps_t[:], func=ACT.Sqrt)
 
+        clk = const.tile([P, 256], F32, name="clk")
+        nc.vector.memset(clk[:], 1.0)
+        praw = const.tile([P, 512], BF16, name="praw")
+        nc.vector.memset(praw[:], 0.0)
         ident_bf = const.tile([P, P], BF16, name="ident_bf")
         make_identity(nc, ident_bf[:])
         ident_f = const.tile([P, P], F32, name="ident_f")
         make_identity(nc, ident_f[:])
-        ones_bf = const.tile([P, N_ONES], BF16, name="ones_bf")
-        nc.vector.memset(ones_bf[:], 1.0)
-        praw = const.tile([P, 512], BF16, name="praw")
-        nc.vector.memset(praw[:], 0.0)
 
         par = const.tile([P, 40], F32, name="par")
         gpair = const.tile([P, MT, 2], F32, name="gpair")
         xq = [const.tile([P, 2 * CH], U32, name="xq%d" % c, align_bytes=64) for c in range(NCH)]
         xsc = [const.tile([P, 2 * CH], U8, name="xsc%d" % c, align_bytes=64) for c in range(NCH)]
-        wq = const.tile([P, 2, DOUT], U32, name="wq", align_bytes=64)
-        wsc = const.tile([P, 2, DOUT], U8, name="wsc", align_bytes=64)
-        st0 = const.tile([P, KB_V, 8, 6], F32, name="st0")
-        mv0 = const.tile([P, KB, 2], F32, name="mv0")
-        nmu = const.tile([P, N_S], F32, name="nmu")
-        sq = const.tile([P, N_S, 8], F32, name="sq")
+        wq = const.tile([P, 2 * DOUT], U32, name="wq", align_bytes=64)
+        wsc = const.tile([P, 2 * DOUT], U8, name="wsc", align_bytes=64)
+        st0 = const.tile([P, 4, NCH, 6], F32, name="st0")
+        mv0 = const.tile([P, 2, 4, 2], F32, name="mv0")
+        ssq = const.tile([P, 4], F32, name="ssq")
+        a0 = const.tile([P, 2, 4], F32, name="a0")
+        nd0 = const.tile([P, 2, 4], F32, name="nd0")
+        nb0 = const.tile([P, 4], F32, name="nb0")
         st1 = [const.tile([P, NCH, 6], F32, name="st1_%d" % m) for m in range(MT)]
         h = {}
 
+        xs = [big.tile([P, 8, K + PAD], BF16, name="xs%d" % q, tag="hx", align_bytes=64) for q in range(4)]
+        for q in range(4):
+            nc.gpsimd.memset(xs[q][:, :, K : K + PAD], 1.0)
+        w_sb = big.tile([P, MT, K], BF16, name="w_sb", tag="ht", align_bytes=64)
+        wg = big.tile([P, 2, 4 * DOUT], BF16, name="wg", tag="ht", align_bytes=64)
+        xT = [big.tile([P, 4, 4 * CH], BF16, name="xT%d" % q, tag="ht", align_bytes=64) for q in range(2)]
+
         ctx.enter_context(tc.manual_schedule())
 
-        def h_tile(q, mh):
-            tag = "hx" if mh == 0 else "ht"
-            h[q, mh] = big.tile([P, 8, 4, P], F32, name="h%d_%d" % (q, mh), tag=tag, align_bytes=64)
+        for i, v in enumerate((g0, b0, c0, g1, b1)):
+            nc.scalar.dma_start(out=praw[2 * i : 2 * i + 2, :], in_=v.rearrange("(g f) -> g f", g=2))
+        for c in range(NCH):
+            j0 = 4 * (c % 2)
+            if c == 0:
+                for jj in range(4):
+                    nc.sync.dma_start(out=xs[0][:, jj : jj + 1, 0:K], in_=x_v[:, jj : jj + 1, :])
+            else:
+                nc.sync.dma_start(out=xs[c // 2][:, j0 : j0 + 4, 0:K], in_=x_v[:, 4 * c : 4 * c + 4, :])
+        for mp in range(4):
+            nc.sync.dma_start(out=w_sb[:, 2 * mp : 2 * mp + 2, :], in_=w_v[:, 2 * mp : 2 * mp + 2, :])
+
+        def feats(g, t, n=P):
+            return slice(512 * g + t, 512 * g + t + 4 * (n - 1) + 1, 4)
+
+        def x_rows(c, jj):
+            return xs[c // 2][:, 4 * (c % 2) + jj, :]
+
+        def x_transposed(c, g, t):
+            pt = ps_t.tile([P, 4, P], BF16, name="pt", tag="tp")
+            for jj in range(4):
+                nc.tensor.transpose(pt[:, jj, :], x_rows(c, jj)[:, feats(g, t)], ident_bf[:])
+            return pt[:].rearrange("p j r -> p (j r)")
+
+        def x_plane(c, t):
+            return xT[c // 4][:, t, (c % 4) * CH : (c % 4 + 1) * CH]
+
+        with tc.psum_pool(name="ps_g", bufs=1) as ps_g:
+            gram = [ps_g.tile([P, NG], F32, name="gram%d" % t) for t in range(4)]
+
+            def grams(c, t):
+                for jj in range(4):
+                    nc.tensor.matmul(
+                        out=gram[t][:], lhsT=x_rows(c, jj)[:, feats(1, t)], rhs=x_rows(c, jj)[:, feats(1, t, NG)],
+                        start=(c == 0 and jj == 0), stop=(c == NCH - 1 and jj == 3),
+                    )
+
+            for n in range(3):
+                pc = ps_t.tile([P, 512], F32, name="pc", tag="tp")
+                nc.tensor.matmul(out=pc[:, 0:256], lhsT=clk[:, 0:P], rhs=clk[:], start=True, stop=True)
+            for c in range(NCH):
+                last = c == NCH - 1
+                if last:
+                    for t in range(4):
+                        grams(c, t)
+                for t in range(4):
+                    src = x_transposed(c, 0, t)
+                    nc.scalar.copy(out=x_plane(c, t), in_=src)
+                    nc.vector.bn_stats(out=st0[:, t, c, :], in_=x_plane(c, t))
+                    if not last:
+                        grams(c, t)
+                    elif t == 1:
+                        for u in range(4):
+                            junk = gpool.tile([P, P], F32, name="junk", tag="junk")
+                            nc.vector.scalar_tensor_tensor(
+                                out=junk[:], in0=gram[u][:, 0:P], scalar=1.0, in1=ident_f[:],
+                                op0=ALU.mult, op1=ALU.mult, accum_out=ssq[:, u : u + 1],
+                            )
+                            nc.vector.tensor_scalar(
+                                out=mv0[:, 1, u, 0:1], in0=gram[u][:, P : P + 1], scalar1=1.0 / ROWS, scalar2=None,
+                                op0=ALU.mult,
+                            )
+                        ms = const.tile([P, 4], F32, name="ms")
+                        nc.vector.tensor_tensor(out=ms[:], in0=mv0[:, 1, :, 0], in1=mv0[:, 1, :, 0], op=ALU.mult)
+                        vr = const.tile([P, 4], F32, name="vr")
+                        nc.vector.scalar_tensor_tensor(
+                            out=vr[:], in0=ssq[:], scalar=1.0 / ROWS, in1=ms[:], op0=ALU.mult, op1=ALU.subtract
+                        )
+                        nc.vector.tensor_scalar(
+                            out=mv0[:, 1, :, 1], in0=vr[:], scalar1=0.0, scalar2=None, op0=ALU.max
+                        )
+                if c == 2:
+                    pps = ps_t.tile([P, 4, P], BF16, name="pps", tag="tp")
+                    for t in range(4):
+                        nc.tensor.transpose(pps[:, t, :], praw[:, feats(0, t)], ident_bf[:])
+                    nc.vector.tensor_copy(
+                        out=par[:, 0:16].rearrange("p (r t) -> p r t", t=4),
+                        in_=pps[:, :, 0:4].rearrange("p t r -> p r t"),
+                    )
+                    ppo = ps_t.tile([P, 4, P], BF16, name="ppo", tag="tp")
+                    for j in range(4):
+                        nc.tensor.transpose(ppo[:, j, :], praw[:, j * P : (j + 1) * P], ident_bf[:])
+                    nc.vector.tensor_copy(
+                        out=par[:, 16:40].rearrange("p (r j) -> p r j", j=4),
+                        in_=ppo[:, :, 4:10].rearrange("p j r -> p r j"),
+                    )
+                    nc.vector.tensor_copy(out=gpair[:, :, 0], in_=par[:, 24:32])
+                    nc.vector.tensor_scalar(
+                        out=gpair[:, :, 1], in0=par[:, 24:32], scalar1=-1.0, scalar2=None, op0=ALU.mult
+                    )
+
+        ps_m = ctx.enter_context(tc.psum_pool(name="ps_m", bufs=4))
+
+        def w_tile(m):
+            words = w_sb[:, m, :].bitcast(F32)
+            pt = ps_m.tile([P, 4, P], F32, name="ptw", tag="acc")
+            for g in range(2):
+                for u in range(2):
+                    lo = 256 * g + u
+                    nc.tensor.transpose(pt[:, 2 * g + u, :], words[:, lo : lo + 2 * (P - 1) + 1 : 2], ident_f[:])
+            nc.scalar.copy(
+                out=wg[:, :, 4 * m * P : 4 * (m + 1) * P].bitcast(F32).rearrange("p g (d u) -> p g d u", u=2),
+                in_=pt[:].rearrange("p (g u) d -> p g d u", u=2),
+            )
+
+        sd0 = const.tile([P, 2, 4], F32, name="sd0")
+        r0 = const.tile([P, 2, 4], F32, name="r0")
+        ma0 = const.tile([P, 2, 4], F32, name="ma0")
+        par_g = par[:, 0:16].rearrange("p (v g t) -> p v g t", v=2, g=2)
+
+        def deviation_x(g):
+            nc.scalar.activation(
+                out=sd0[:, g, :], in_=mv0[:, g, :, 1], func=ACT.Sqrt, bias=eps_t[:, 0:1], scale=1.0
+            )
+
+        def scales_x(g):
+            nc.vector.reciprocal(out=r0[:, g, :], in_=sd0[:, g, :])
+            nc.vector.tensor_tensor(out=a0[:, g, :], in0=r0[:, g, :], in1=par_g[:, 0, g, :], op=ALU.mult)
+            nc.vector.tensor_tensor(out=ma0[:, g, :], in0=mv0[:, g, :, 0], in1=a0[:, g, :], op=ALU.mult)
+            nc.vector.tensor_tensor(out=nd0[:, g, :], in0=ma0[:, g, :], in1=par_g[:, 1, g, :], op=ALU.subtract)
+
+        deviation_x(1)
+        for t in range(4):
+            nc.vector.bn_aggr(out=mv0[:, 0, t, :], in_=st0[:, t, :, :].rearrange("p c s -> p (c s)"))
+        deviation_x(0)
+        scales_x(1)
+        nc.vector.tensor_scalar(out=nb0[:], in0=nd0[:, 1, :], scalar1=-1.0, scalar2=None, op0=ALU.mult)
+        scales_x(0)
 
         def h_part(m, c):
             return h[c // 2, m // 4][:, 4 * (c % 2) : 4 * (c % 2) + 4, m % 4, :]
 
-        def mx(pool, m, c):
-            if (c // 2, m // 4) not in h:
-                h_tile(c // 2, m // 4)
-            acc = pool.tile([P, 4, P], F32, name="acc", tag="acc")
+        def mx(m, c):
+            key = (c // 2, m // 4)
+            if key not in h:
+                tag = "hx" if key[1] == 0 else "ht"
+                h[key] = big.tile([P, 8, 4, P], F32, name="h%d_%d" % key, tag=tag, align_bytes=64)
+            acc = ps_m.tile([P, 4, P], F32, name="acc", tag="acc")
             for g in range(2):
+                lo = g * DOUT + m * P
                 nc.tensor.matmul_mx(
                     out=acc[:].rearrange("p j r -> p (j r)"),
-                    lhsT=wq[:, g, m * P : (m + 1) * P].bitcast(FP8X4),
-                    lhsT_scale=wsc[:, g, m * P : (m + 1) * P],
+                    lhsT=wq[:, lo : lo + P].bitcast(FP8X4),
+                    lhsT_scale=wsc[:, lo : lo + P],
                     rhs=xq[c][:, g * CH : (g + 1) * CH].bitcast(FP8X4),
                     rhs_scale=xsc[c][:, g * CH : (g + 1) * CH],
                     start=(g == 0),
@@ -102,182 +240,75 @@ def tile_settransform_pa_t_kernel(tc, set_feats, g0, b0, W0, c0, g1, b1, out):
         def bn(m, c):
             nc.vector.bn_stats(out=st1[m][:, c, :], in_=h_part(m, c))
 
-        with ExitStack() as actx:
-            wpool = actx.enter_context(tc.tile_pool(name="wpool", bufs=1))
-            gpool = actx.enter_context(tc.tile_pool(name="gpool", bufs=4))
-            jpool = actx.enter_context(tc.tile_pool(name="jpool", bufs=2))
+        gr = {}
+        xn = {}
+        pts = {}
 
-            for i, v in enumerate((g0, b0, c0, g1, b1)):
-                nc.scalar.dma_start(out=praw[2 * i : 2 * i + 2, :], in_=v.rearrange("(g f) -> g f", g=2))
-
-            xs = [big.tile([P, 8, K], BF16, name="xs%d" % q, tag="hx", align_bytes=64) for q in range(4)]
-            xT = [big.tile([P, KB, 1024], BF16, name="xT%d" % q, tag="ht", align_bytes=64) for q in range(4)]
-            w_sb = wpool.tile([P, MT, K], BF16, name="w_sb")
-            wg = [gpool.tile([P, 4 * DOUT], BF16, name="wg%d" % g, tag="gr", align_bytes=64) for g in range(2)]
-
-            with ExitStack() as pctx:
-                ps_a = pctx.enter_context(tc.psum_pool(name="ps_a", bufs=6))
-                ps_s = pctx.enter_context(tc.psum_pool(name="ps_s", bufs=1))
-                sums = [ps_s.tile([P, N_ONES], F32, name="sums%d" % i) for i in range(N_S)]
-                first = ps_a.tile([P, N_S, 32], F32, name="first", tag="tp")
-
-                def feats(kb):
-                    g, t = kb // 4, kb % 4
-                    return slice(512 * g + t, 512 * g + t + 4 * (P - 1) + 1, 4)
-
-                def w_tile(m):
-                    words = w_sb[:, m, :].bitcast(F32)
-                    pt = ps_a.tile([P, 2, 2, P], F32, name="ptw", tag="tp")
-                    for g in range(2):
-                        for u in range(2):
-                            lo = 256 * g + u
-                            nc.tensor.transpose(pt[:, g, u, :], words[:, lo : lo + 2 * (P - 1) + 1 : 2], ident_f[:])
-                    for g in range(2):
-                        nc.scalar.copy(
-                            out=wg[g][:, 4 * m * P : 4 * (m + 1) * P].bitcast(F32).rearrange("p (d u) -> p d u", u=2),
-                            in_=pt[:, g, :, :].rearrange("p u d -> p d u"),
-                        )
-
-                for c in range(NCH):
-                    j0 = 4 * (c % 2)
-                    x_sb = xs[c // 2][:, j0 : j0 + 4, :]
-                    if c == 0:
-                        for hk in range(2):
-                            nc.sync.dma_start(
-                                out=x_sb[:, :, hk * 512 : (hk + 1) * 512], in_=x_v[:, 0:4, hk * 512 : (hk + 1) * 512]
-                            )
-                    else:
-                        nc.sync.dma_start(out=x_sb, in_=x_v[:, 4 * c : 4 * c + 4, :])
-                    if c == 3:
-                        nc.sync.dma_start(out=w_sb[:], in_=w_v)
-                    base = (c % 2) * CH
-                    if c == 0:
-                        for i in range(N_S):
-                            nc.tensor.matmul(
-                                out=first[:, i, :], lhsT=x_sb[:, 0, feats(i)], rhs=ones_bf[:, 0:32],
-                                start=True, stop=True,
-                            )
-                        nc.scalar.activation(out=nmu[:], in_=first[:, :, 0], func=ACT.Copy, scale=-1.0 / P)
-                    for kb in range(KB):
-                        pt = ps_a.tile([P, 4, P], BF16, name="pt", tag="tp")
-                        for jj in range(4):
-                            nc.tensor.transpose(pt[:, jj, :], x_sb[:, jj, feats(kb)], ident_bf[:])
-                        i, jj = kb // 4, kb % 4
-                        nc.tensor.matmul(
-                            out=sums[i][:], lhsT=x_sb[:, jj, feats(i)], rhs=ones_bf[:],
-                            start=(c == 0 and jj == 0), stop=(c == 7 and jj == 3),
-                        )
-                        dst = xT[c // 2][:, kb, base : base + CH]
-                        nc.scalar.copy(out=dst, in_=pt[:].rearrange("p j r -> p (j r)"))
-                        if kb >= N_S:
-                            nc.vector.bn_stats(out=st0[:, kb - N_S, c, :], in_=dst)
-                        if kb in (3, 6):
-                            i = kb // 3 - 1
-                            junk = jpool.tile([P, CH], BF16, name="junk", tag="junk")
-                            nc.scalar.activation(
-                                out=junk[:], in_=xT[c // 2][:, i, base : base + CH], func=ACT.Square,
-                                bias=nmu[:, i : i + 1], scale=1.0, accum_out=sq[:, i, c : c + 1],
-                            )
-                    if c == 2:
-                        pps = ps_a.tile([P, 4, P], BF16, name="pps", tag="tp")
-                        for t in range(4):
-                            nc.tensor.transpose(pps[:, t, :], praw[:, t : t + 4 * (P - 1) + 1 : 4], ident_bf[:])
-                        nc.vector.tensor_copy(
-                            out=par[:, 0:16].rearrange("p (r t) -> p r t", t=4),
-                            in_=pps[:, :, 0:4].rearrange("p t r -> p r t"),
-                        )
-                        ppo = ps_a.tile([P, 4, P], BF16, name="ppo", tag="tp")
-                        for j in range(4):
-                            nc.tensor.transpose(ppo[:, j, :], praw[:, j * P : (j + 1) * P], ident_bf[:])
-                        nc.vector.tensor_copy(
-                            out=par[:, 16:40].rearrange("p (r j) -> p r j", j=4),
-                            in_=ppo[:, :, 4:10].rearrange("p j r -> p r j"),
-                        )
-                        nc.vector.tensor_copy(out=gpair[:, :, 0], in_=par[:, 24:32])
-                        nc.vector.tensor_scalar(
-                            out=gpair[:, :, 1], in0=par[:, 24:32], scalar1=-1.0, scalar2=None, op0=ALU.mult
-                        )
-
-                w_tile(0)
-                for kb in range(N_S, KB):
-                    nc.vector.bn_aggr(out=mv0[:, kb, :], in_=st0[:, kb - N_S, :, :].rearrange("p c s -> p (c s)"))
-                for i in range(N_S):
-                    nc.vector.tensor_scalar(
-                        out=mv0[:, i, 0:1], in0=sums[i][:, 0:1], scalar1=1.0 / ROWS, scalar2=None, op0=ALU.mult
-                    )
-                sqs = const.tile([P, N_S], F32, name="sqs")
-                nc.vector.tensor_reduce(out=sqs[:], in_=sq[:], axis=AX.X, op=ALU.add)
-                dl = const.tile([P, N_S], F32, name="dl")
-                nc.vector.tensor_tensor(out=dl[:], in0=mv0[:, 0:N_S, 0], in1=nmu[:], op=ALU.add)
-                dl2 = const.tile([P, N_S], F32, name="dl2")
-                nc.vector.tensor_tensor(out=dl2[:], in0=dl[:], in1=dl[:], op=ALU.mult)
-                nc.vector.scalar_tensor_tensor(
-                    out=mv0[:, 0:N_S, 1], in0=sqs[:], scalar=1.0 / ROWS, in1=dl2[:], op0=ALU.mult, op1=ALU.subtract
+        def normalise_x(c):
+            for t in range(4):
+                nc.vector.tensor_scalar(
+                    out=x_plane(c, t), in0=x_plane(c, t), scalar1=a0[:, 0, t : t + 1], scalar2=nd0[:, 0, t : t + 1],
+                    op0=ALU.mult, op1=ALU.subtract,
                 )
-                w_tile(1)
-                w_tile(2)
-                sd0 = const.tile([P, KB], F32, name="sd0")
-                nc.scalar.activation(out=sd0[:], in_=mv0[:, :, 1], func=ACT.Sqrt, bias=eps_t[:, 0:1], scale=1.0)
-                for m in range(3, MT):
-                    w_tile(m)
-                r0 = const.tile([P, KB], F32, name="r0")
-                nc.vector.reciprocal(out=r0[:], in_=sd0[:])
-                a0 = const.tile([P, KB], F32, name="a0")
-                nc.vector.tensor_tensor(out=a0[:], in0=r0[:], in1=par[:, 0:8], op=ALU.mult)
-                ma0 = const.tile([P, KB], F32, name="ma0")
-                nc.vector.tensor_tensor(out=ma0[:], in0=mv0[:, :, 0], in1=a0[:], op=ALU.mult)
-                nd0 = const.tile([P, KB], F32, name="nd0")
-                nc.vector.tensor_tensor(out=nd0[:], in0=ma0[:], in1=par[:, 8:16], op=ALU.subtract)
-
-            ps_t = ctx.enter_context(tc.psum_pool(name="ps_t", bufs=4))
-            ps_m = ctx.enter_context(tc.psum_pool(name="ps_m", bufs=4))
-            gr = {}
-
-            def normalise_x(c):
-                base = (c % 2) * CH
-                for kb in range(KB):
-                    xs_ = xT[c // 2][:, kb, base : base + CH]
+            for t in range(4):
+                dst = xn[c][:, t, :]
+                if t % 2 == 0:
                     nc.vector.tensor_scalar(
-                        out=xs_, in0=xs_, scalar1=a0[:, kb : kb + 1], scalar2=nd0[:, kb : kb + 1],
+                        out=dst, in0=pts[c][t], scalar1=a0[:, 1, t : t + 1], scalar2=nd0[:, 1, t : t + 1],
                         op0=ALU.mult, op1=ALU.subtract,
                     )
-
-            def regroup(c, g, lo, hi, on_scalar):
-                base = (c % 2) * CH
-                src = xT[c // 2][:, 4 * g : 4 * g + 4, base + lo : base + hi].rearrange("p t (c i) -> p c t i", i=4)
-                dst = gr[c][:, 4 * (g * CH + lo) : 4 * (g * CH + hi)].rearrange("p (c i t) -> p c t i", i=4, t=4)
-                if on_scalar:
-                    nc.scalar.copy(out=dst, in_=src)
                 else:
-                    nc.vector.tensor_copy(out=dst, in_=src)
+                    nc.scalar.activation(
+                        out=dst, in_=pts[c][t], func=ACT.Identity, bias=nb0[:, t : t + 1], scale=a0[:, 1, t : t + 1]
+                    )
 
-            def quantise_x(c):
-                nc.vector.quantize_mx(out=xq[c][:].bitcast(FP8X4), scales=xsc[c][:], in_=gr[c][:])
+        def regroup(c, g, lo, hi, on_scalar):
+            if g == 0:
+                src = xT[c // 4][:, :, (c % 4) * CH + lo : (c % 4) * CH + hi]
+            else:
+                src = xn[c][:, :, lo:hi]
+            src = src.rearrange("p t (c i) -> p c t i", i=4)
+            dst = gr[c][:, 4 * (g * CH + lo) : 4 * (g * CH + hi)].rearrange("p (c i t) -> p c t i", i=4, t=4)
+            if on_scalar:
+                nc.scalar.copy(out=dst, in_=src)
+            else:
+                nc.vector.tensor_copy(out=dst, in_=src)
 
-            for i in range(NCH + 1):
-                if i < NCH:
-                    gr[i] = gpool.tile([P, 8 * CH], BF16, name="gr", tag="gr", align_bytes=64)
-                    normalise_x(i)
-                if i == 1:
-                    for g in range(2):
-                        nc.vector.quantize_mx(out=wq[:, g, :].bitcast(FP8X4), scales=wsc[:, g, :], in_=wg[g][:])
-                if 1 <= i <= NCH:
-                    quantise_x(i - 1)
-                if i < NCH:
-                    cut = CH if i == 0 else (0 if i == 1 else 3 * CH // 4)
-                    regroup(i, 0, 0, CH, False)
-                    if cut > 0:
-                        regroup(i, 1, 0, cut, False)
-                    if cut < CH:
-                        regroup(i, 1, cut, CH, True)
-                if 1 <= i <= NCH:
-                    for m in range(MT):
-                        relu(m, i - 1, mx(ps_m, m, i - 1))
-                if 2 <= i <= NCH:
-                    bn(0, i - 2)
-            for c in range(4):
-                bn(1, c)
-            bn(0, NCH - 1)
+        def quantise_x(c):
+            nc.vector.quantize_mx(out=xq[c][:].bitcast(FP8X4), scales=xsc[c][:], in_=gr[c][:])
+
+        pts[0] = [x_transposed(0, 1, t) for t in range(4)]
+        for i in range(NCH + 1):
+            if i < NCH:
+                gr[i] = gpool.tile([P, 8 * CH], BF16, name="gr", tag="gr", align_bytes=64)
+                xn[i] = gpool.tile([P, 4, CH], BF16, name="xn", tag="xn", align_bytes=64)
+                normalise_x(i)
+            if i == 0:
+                for m in range(MT):
+                    w_tile(m)
+            if i == 1:
+                for g in range(2):
+                    cols = slice(g * DOUT, (g + 1) * DOUT)
+                    nc.vector.quantize_mx(out=wq[:, cols].bitcast(FP8X4), scales=wsc[:, cols], in_=wg[:, g, :])
+            if i >= 1:
+                quantise_x(i - 1)
+            if i < NCH:
+                cut = CH if i == 0 else (0 if i == 1 else 3 * CH // 4)
+                regroup(i, 0, 0, CH, False)
+                if cut > 0:
+                    regroup(i, 1, 0, cut, False)
+                if cut < CH:
+                    regroup(i, 1, cut, CH, True)
+            if i + 1 < NCH:
+                pts[i + 1] = [x_transposed(i + 1, 1, t) for t in range(4)]
+            if i >= 1:
+                for m in range(NM2):
+                    relu(m, i - 1, mx(m, i - 1))
+            if 2 <= i <= NCH:
+                bn(0, i - 2)
+        for c in range(2):
+            bn(1, c)
+        bn(0, NCH - 1)
 
         stats = {}
 
@@ -337,10 +368,18 @@ def tile_settransform_pa_t_kernel(tc, set_feats, g0, b0, W0, c0, g1, b1, out):
 
         close_stats(0)
         deviation(0)
+        n_late = 4 * (MT - NM2)
         for k in range(2 * MT + LAG):
             mb, hb = 1 + k // 2, k % 2
-            chunks = range(4 * hb, 4 * hb + 4) if mb < MT and k > 0 else ()
+            chunks = range(4 * hb, 4 * hb + 4) if mb < MT else ()
+            if k == 0:
+                chunks = range(2, 4)
             tail = mb >= MT
+            if k < n_late:
+                ml, cl = NM2 + k // 4, 2 * (k % 4)
+                accs = [mx(ml, cl + n) for n in range(2)]
+                for n in range(2):
+                    relu(ml, cl + n, accs[n])
             banks = []
             if hb == 0 and 0 < k and mb <= MT:
                 deviation(mb - 1)
@@ -359,4 +398,4 @@ def tile_settransform_pa_t_kernel(tc, set_feats, g0, b0, W0, c0, g1, b1, out):
                 close_stats(mb)
             if banks:
                 evac(mt, 4 * th + 2, banks[2], False)
-                evac(mt, 4 * th + 3, banks[3], tail)
+                evac(mt, 4 * th + 3, banks[3], tail or th == 1)

@@ -23,8 +23,7 @@ NCH = ROWS // CH
 EPS = 1e-5
 FLOPS = 2 * ROWS * K * DOUT
 
-PAD = 8
-NG = P + 2
+N_SUM = 16
 NM2 = 5
 STORE_GROUPS = ((0, 1), (2, 3), (4, 5), (6,), (7,))
 LAG = 1
@@ -41,21 +40,30 @@ def tile_settransform_pa_t_kernel(tc, set_feats, g0, b0, W0, c0, g1, b1, out):
         big = ctx.enter_context(tc.tile_pool(name="big", bufs=4))
         gpool = ctx.enter_context(tc.tile_pool(name="gpool", bufs=3))
         small = ctx.enter_context(tc.tile_pool(name="small", bufs=3))
-        ps_t = ctx.enter_context(tc.psum_pool(name="ps_t", bufs=4))
+        ps_t = ctx.enter_context(tc.psum_pool(name="ps_t", bufs=3))
 
         eps_t = const.tile([P, 1], F32, name="eps_t")
         nc.vector.memset(eps_t[:], EPS)
         warm = const.tile([P, 1], F32, name="warm")
         nc.scalar.activation(out=warm[:], in_=eps_t[:], func=ACT.Sqrt)
 
-        clk = const.tile([P, 256], F32, name="clk")
-        nc.vector.memset(clk[:], 1.0)
         praw = const.tile([P, 512], BF16, name="praw")
         nc.vector.memset(praw[:], 0.0)
-        ident_bf = const.tile([P, P], BF16, name="ident_bf")
-        make_identity(nc, ident_bf[:])
         ident_f = const.tile([P, P], F32, name="ident_f")
         make_identity(nc, ident_f[:])
+        ident_bf = const.tile([P, P], BF16, name="ident_bf")
+        nc.vector.tensor_copy(out=ident_bf[:], in_=ident_f[:])
+        hot = const.tile([P, 4, N_SUM], BF16, name="hot")
+        nc.vector.memset(hot[:], 0.0)
+        for b in range(4):
+            nc.vector.memset(hot[:, b, b : b + 1], 1.0)
+        sel = const.tile([P, 4, P], F32, name="sel")
+        quad = const.tile([P, 8, 4], F32, name="quad")
+        nc.vector.memset(quad[:], 0.0)
+        for b in range(4):
+            nc.vector.memset(quad[32 * b : 32 * b + 32, :, b : b + 1], 1.0)
+            for t in range(4):
+                nc.vector.tensor_copy(out=sel[:, t, 32 * b : 32 * b + 32], in_=ident_f[:, t : t + 125 : 4])
 
         par = const.tile([P, 40], F32, name="par")
         gpair = const.tile([P, MT, 2], F32, name="gpair")
@@ -65,16 +73,16 @@ def tile_settransform_pa_t_kernel(tc, set_feats, g0, b0, W0, c0, g1, b1, out):
         wsc = const.tile([P, 2 * DOUT], U8, name="wsc", align_bytes=64)
         st0 = const.tile([P, 4, NCH, 6], F32, name="st0")
         mv0 = const.tile([P, 2, 4, 2], F32, name="mv0")
-        ssq = const.tile([P, 4], F32, name="ssq")
+        nat = const.tile([P, 2, 4], F32, name="nat")
+        srt = const.tile([P, 8, 4], F32, name="srt")
+        raw = const.tile([P, 4, 2], F32, name="raw")
         a0 = const.tile([P, 2, 4], F32, name="a0")
         nd0 = const.tile([P, 2, 4], F32, name="nd0")
         nb0 = const.tile([P, 4], F32, name="nb0")
         st1 = [const.tile([P, NCH, 6], F32, name="st1_%d" % m) for m in range(MT)]
         h = {}
 
-        xs = [big.tile([P, 8, K + PAD], BF16, name="xs%d" % q, tag="hx", align_bytes=64) for q in range(4)]
-        for q in range(4):
-            nc.gpsimd.memset(xs[q][:, :, K : K + PAD], 1.0)
+        xs = [big.tile([P, 8, K], BF16, name="xs%d" % q, tag="hx", align_bytes=64) for q in range(4)]
         w_sb = big.tile([P, MT, K], BF16, name="w_sb", tag="ht", align_bytes=64)
         wg = big.tile([P, 2, 4 * DOUT], BF16, name="wg", tag="ht", align_bytes=64)
         xT = [big.tile([P, 4, 4 * CH], BF16, name="xT%d" % q, tag="ht", align_bytes=64) for q in range(2)]
@@ -83,108 +91,49 @@ def tile_settransform_pa_t_kernel(tc, set_feats, g0, b0, W0, c0, g1, b1, out):
 
         for i, v in enumerate((g0, b0, c0, g1, b1)):
             nc.scalar.dma_start(out=praw[2 * i : 2 * i + 2, :], in_=v.rearrange("(g f) -> g f", g=2))
+        for mp in range(4):
+            nc.sync.dma_start(out=w_sb[:, 2 * mp : 2 * mp + 2, :], in_=w_v[:, 2 * mp : 2 * mp + 2, :])
         for c in range(NCH):
             j0 = 4 * (c % 2)
             if c == 0:
                 for jj in range(4):
-                    nc.sync.dma_start(out=xs[0][:, jj : jj + 1, 0:K], in_=x_v[:, jj : jj + 1, :])
+                    nc.sync.dma_start(out=xs[0][:, jj : jj + 1, :], in_=x_v[:, jj : jj + 1, :])
             else:
-                nc.sync.dma_start(out=xs[c // 2][:, j0 : j0 + 4, 0:K], in_=x_v[:, 4 * c : 4 * c + 4, :])
-        for mp in range(4):
-            nc.sync.dma_start(out=w_sb[:, 2 * mp : 2 * mp + 2, :], in_=w_v[:, 2 * mp : 2 * mp + 2, :])
-
-        def feats(g, t, n=P):
-            return slice(512 * g + t, 512 * g + t + 4 * (n - 1) + 1, 4)
+                nc.sync.dma_start(out=xs[c // 2][:, j0 : j0 + 4, :], in_=x_v[:, 4 * c : 4 * c + 4, :])
 
         def x_rows(c, jj):
             return xs[c // 2][:, 4 * (c % 2) + jj, :]
 
-        def x_transposed(c, g, t):
-            pt = ps_t.tile([P, 4, P], BF16, name="pt", tag="tp")
+        def word_columns(g, u):
+            return slice(256 * g + u, 256 * g + u + 2 * (P - 1) + 1, 2)
+
+        def x_transposed(c, g, u):
+            pt = ps_t.tile([P, 4, P], F32, name="pt", tag="tp")
             for jj in range(4):
-                nc.tensor.transpose(pt[:, jj, :], x_rows(c, jj)[:, feats(g, t)], ident_bf[:])
-            return pt[:].rearrange("p j r -> p (j r)")
+                nc.tensor.transpose(pt[:, jj, :], x_rows(c, jj).bitcast(F32)[:, word_columns(g, u)], ident_f[:])
+            return pt[:].rearrange("p j r -> p (j r)").bitcast(BF16).rearrange("p (r e) -> p e r", e=2)
 
-        def x_plane(c, t):
-            return xT[c // 4][:, t, (c % 4) * CH : (c % 4 + 1) * CH]
-
-        with tc.psum_pool(name="ps_g", bufs=1) as ps_g:
-            gram = [ps_g.tile([P, NG], F32, name="gram%d" % t) for t in range(4)]
-
-            def grams(c, t):
-                for jj in range(4):
-                    nc.tensor.matmul(
-                        out=gram[t][:], lhsT=x_rows(c, jj)[:, feats(1, t)], rhs=x_rows(c, jj)[:, feats(1, t, NG)],
-                        start=(c == 0 and jj == 0), stop=(c == NCH - 1 and jj == 3),
-                    )
-
-            for n in range(3):
-                pc = ps_t.tile([P, 512], F32, name="pc", tag="tp")
-                nc.tensor.matmul(out=pc[:, 0:256], lhsT=clk[:, 0:P], rhs=clk[:], start=True, stop=True)
-            for c in range(NCH):
-                last = c == NCH - 1
-                if last:
-                    for t in range(4):
-                        grams(c, t)
-                for t in range(4):
-                    src = x_transposed(c, 0, t)
-                    nc.scalar.copy(out=x_plane(c, t), in_=src)
-                    nc.vector.bn_stats(out=st0[:, t, c, :], in_=x_plane(c, t))
-                    if not last:
-                        grams(c, t)
-                    elif t == 1:
-                        for u in range(4):
-                            junk = gpool.tile([P, P], F32, name="junk", tag="junk")
-                            nc.vector.scalar_tensor_tensor(
-                                out=junk[:], in0=gram[u][:, 0:P], scalar=1.0, in1=ident_f[:],
-                                op0=ALU.mult, op1=ALU.mult, accum_out=ssq[:, u : u + 1],
-                            )
-                            nc.vector.tensor_scalar(
-                                out=mv0[:, 1, u, 0:1], in0=gram[u][:, P : P + 1], scalar1=1.0 / ROWS, scalar2=None,
-                                op0=ALU.mult,
-                            )
-                        ms = const.tile([P, 4], F32, name="ms")
-                        nc.vector.tensor_tensor(out=ms[:], in0=mv0[:, 1, :, 0], in1=mv0[:, 1, :, 0], op=ALU.mult)
-                        vr = const.tile([P, 4], F32, name="vr")
-                        nc.vector.scalar_tensor_tensor(
-                            out=vr[:], in0=ssq[:], scalar=1.0 / ROWS, in1=ms[:], op0=ALU.mult, op1=ALU.subtract
-                        )
-                        nc.vector.tensor_scalar(
-                            out=mv0[:, 1, :, 1], in0=vr[:], scalar1=0.0, scalar2=None, op0=ALU.max
-                        )
-                if c == 2:
-                    pps = ps_t.tile([P, 4, P], BF16, name="pps", tag="tp")
-                    for t in range(4):
-                        nc.tensor.transpose(pps[:, t, :], praw[:, feats(0, t)], ident_bf[:])
-                    nc.vector.tensor_copy(
-                        out=par[:, 0:16].rearrange("p (r t) -> p r t", t=4),
-                        in_=pps[:, :, 0:4].rearrange("p t r -> p r t"),
-                    )
-                    ppo = ps_t.tile([P, 4, P], BF16, name="ppo", tag="tp")
-                    for j in range(4):
-                        nc.tensor.transpose(ppo[:, j, :], praw[:, j * P : (j + 1) * P], ident_bf[:])
-                    nc.vector.tensor_copy(
-                        out=par[:, 16:40].rearrange("p (r j) -> p r j", j=4),
-                        in_=ppo[:, :, 4:10].rearrange("p j r -> p r j"),
-                    )
-                    nc.vector.tensor_copy(out=gpair[:, :, 0], in_=par[:, 24:32])
-                    nc.vector.tensor_scalar(
-                        out=gpair[:, :, 1], in0=par[:, 24:32], scalar1=-1.0, scalar2=None, op0=ALU.mult
-                    )
-
-        ps_m = ctx.enter_context(tc.psum_pool(name="ps_m", bufs=4))
+        def x_planes(c, t0, t1):
+            return xT[c // 4][:, t0:t1, (c % 4) * CH : (c % 4 + 1) * CH]
 
         def w_tile(m):
             words = w_sb[:, m, :].bitcast(F32)
-            pt = ps_m.tile([P, 4, P], F32, name="ptw", tag="acc")
+            pt = ps_t.tile([P, 4, P], F32, name="ptw", tag="tp")
             for g in range(2):
                 for u in range(2):
-                    lo = 256 * g + u
-                    nc.tensor.transpose(pt[:, 2 * g + u, :], words[:, lo : lo + 2 * (P - 1) + 1 : 2], ident_f[:])
-            nc.scalar.copy(
-                out=wg[:, :, 4 * m * P : 4 * (m + 1) * P].bitcast(F32).rearrange("p g (d u) -> p g d u", u=2),
-                in_=pt[:].rearrange("p (g u) d -> p g d u", u=2),
-            )
+                    nc.tensor.transpose(pt[:, 2 * g + u, :], words[:, word_columns(g, u)], ident_f[:])
+            dst = wg[:, :, 4 * m * P : 4 * (m + 1) * P].bitcast(F32).rearrange("p g (d u) -> p g d u", u=2)
+            src = pt[:].rearrange("p (g u) d -> p g d u", u=2)
+            if m % 2 == 0:
+                nc.scalar.copy(out=dst, in_=src)
+            else:
+                nc.vector.tensor_copy(out=dst, in_=src)
+
+        for m in range(MT):
+            w_tile(m)
+        for g in range(2):
+            cols = slice(g * DOUT, (g + 1) * DOUT)
+            nc.vector.quantize_mx(out=wq[:, cols].bitcast(FP8X4), scales=wsc[:, cols], in_=wg[:, g, :])
 
         sd0 = const.tile([P, 2, 4], F32, name="sd0")
         r0 = const.tile([P, 2, 4], F32, name="r0")
@@ -202,12 +151,96 @@ def tile_settransform_pa_t_kernel(tc, set_feats, g0, b0, W0, c0, g1, b1, out):
             nc.vector.tensor_tensor(out=ma0[:, g, :], in0=mv0[:, g, :, 0], in1=a0[:, g, :], op=ALU.mult)
             nc.vector.tensor_tensor(out=nd0[:, g, :], in0=ma0[:, g, :], in1=par_g[:, 1, g, :], op=ALU.subtract)
 
-        deviation_x(1)
+        def sorted_sums():
+            pr = ps_t.tile([P, 4, 8], F32, name="pr", tag="tp")
+            for t in range(4):
+                nc.tensor.matmul(
+                    out=pr[:, t, :], lhsT=sel[:, t, :], rhs=nat[:].rearrange("p s b -> p (s b)"), start=True, stop=True
+                )
+            nc.vector.tensor_tensor(
+                out=srt[:], in0=pr[:].rearrange("p t (s b) -> p (t s) b", b=4), in1=quad[:], op=ALU.mult
+            )
+            nc.vector.tensor_reduce(
+                out=raw[:].rearrange("p t s -> p (t s)"), in_=srt[:], axis=mybir.AxisListType.X, op=ALU.add
+            )
+            nc.vector.tensor_scalar(
+                out=mv0[:, 1, :, 0], in0=raw[:, :, 1], scalar1=1.0 / ROWS, scalar2=None, op0=ALU.mult
+            )
+            ms = const.tile([P, 4], F32, name="ms")
+            nc.vector.tensor_tensor(out=ms[:], in0=mv0[:, 1, :, 0], in1=mv0[:, 1, :, 0], op=ALU.mult)
+            vr = const.tile([P, 4], F32, name="vr")
+            nc.vector.scalar_tensor_tensor(
+                out=vr[:], in0=raw[:, :, 0], scalar=1.0 / ROWS, in1=ms[:], op0=ALU.mult, op1=ALU.subtract
+            )
+            nc.vector.tensor_scalar(out=mv0[:, 1, :, 1], in0=vr[:], scalar1=0.0, scalar2=None, op0=ALU.max)
+
+        with tc.psum_pool(name="ps_g", bufs=1) as ps_g:
+            gram = [ps_g.tile([P, P], F32, name="gram%d" % b) for b in range(4)]
+            sums = ps_g.tile([P, N_SUM], F32, name="sums")
+
+            def natural_sums():
+                for b in range(4):
+                    junk = gpool.tile([P, P], F32, name="junk", tag="junk")
+                    nc.vector.scalar_tensor_tensor(
+                        out=junk[:], in0=gram[b][:], scalar=1.0, in1=ident_f[:],
+                        op0=ALU.mult, op1=ALU.mult, accum_out=nat[:, 0, b : b + 1],
+                    )
+                nc.vector.tensor_copy(out=nat[:, 1, :], in_=sums[:, 0:4])
+
+            def grams(c, b):
+                for jj in range(4):
+                    x_b = x_rows(c, jj)[:, 512 + P * b : 512 + P * (b + 1)]
+                    first, last = c == 0 and jj == 0, c == NCH - 1 and jj == 3
+                    nc.tensor.matmul(out=gram[b][:], lhsT=x_b, rhs=x_b, start=first, stop=last)
+                    nc.tensor.matmul(
+                        out=sums[:], lhsT=x_b, rhs=hot[:, b, :], start=first and b == 0, stop=last and b == 3
+                    )
+
+            for c in range(NCH):
+                last = c == NCH - 1
+                if last:
+                    for b in range(4):
+                        grams(c, b)
+                for u in range(2):
+                    src = x_transposed(c, 0, u)
+                    nc.scalar.copy(out=x_planes(c, 2 * u, 2 * u + 2), in_=src)
+                    if not last:
+                        grams(c, 2 * u)
+                        grams(c, 2 * u + 1)
+                    elif u == 0:
+                        natural_sums()
+                    else:
+                        sorted_sums()
+                        deviation_x(1)
+                    for t in (2 * u, 2 * u + 1):
+                        nc.vector.bn_stats(out=st0[:, t, c, :], in_=x_planes(c, t, t + 1)[:, 0, :])
+                if c == 2:
+                    pps = ps_t.tile([P, 4, P], BF16, name="pps", tag="tp")
+                    for t in range(4):
+                        nc.tensor.transpose(pps[:, t, :], praw[:, t : t + 4 * (P - 1) + 1 : 4], ident_bf[:])
+                    nc.vector.tensor_copy(
+                        out=par[:, 0:16].rearrange("p (r t) -> p r t", t=4),
+                        in_=pps[:, :, 0:4].rearrange("p t r -> p r t"),
+                    )
+                    ppo = ps_t.tile([P, 4, P], BF16, name="ppo", tag="tp")
+                    for j in range(4):
+                        nc.tensor.transpose(ppo[:, j, :], praw[:, j * P : (j + 1) * P], ident_bf[:])
+                    nc.vector.tensor_copy(
+                        out=par[:, 16:40].rearrange("p (r j) -> p r j", j=4),
+                        in_=ppo[:, :, 4:10].rearrange("p j r -> p r j"),
+                    )
+                    nc.vector.tensor_copy(out=gpair[:, :, 0], in_=par[:, 24:32])
+                    nc.vector.tensor_scalar(
+                        out=gpair[:, :, 1], in0=par[:, 24:32], scalar1=-1.0, scalar2=None, op0=ALU.mult
+                    )
+
+        ps_m = ctx.enter_context(tc.psum_pool(name="ps_m", bufs=5))
+
         for t in range(4):
             nc.vector.bn_aggr(out=mv0[:, 0, t, :], in_=st0[:, t, :, :].rearrange("p c s -> p (c s)"))
-        deviation_x(0)
         scales_x(1)
         nc.vector.tensor_scalar(out=nb0[:], in0=nd0[:, 1, :], scalar1=-1.0, scalar2=None, op0=ALU.mult)
+        deviation_x(0)
         scales_x(0)
 
         def h_part(m, c):
@@ -244,63 +277,46 @@ def tile_settransform_pa_t_kernel(tc, set_feats, g0, b0, W0, c0, g1, b1, out):
         xn = {}
         pts = {}
 
-        def normalise_x(c):
+        def normalise_first(c):
             for t in range(4):
+                plane = x_planes(c, t, t + 1)[:, 0, :]
                 nc.vector.tensor_scalar(
-                    out=x_plane(c, t), in0=x_plane(c, t), scalar1=a0[:, 0, t : t + 1], scalar2=nd0[:, 0, t : t + 1],
+                    out=plane, in0=plane, scalar1=a0[:, 0, t : t + 1], scalar2=nd0[:, 0, t : t + 1],
                     op0=ALU.mult, op1=ALU.subtract,
                 )
-            for t in range(4):
-                dst = xn[c][:, t, :]
-                if t % 2 == 0:
-                    nc.vector.tensor_scalar(
-                        out=dst, in0=pts[c][t], scalar1=a0[:, 1, t : t + 1], scalar2=nd0[:, 1, t : t + 1],
-                        op0=ALU.mult, op1=ALU.subtract,
-                    )
-                else:
-                    nc.scalar.activation(
-                        out=dst, in_=pts[c][t], func=ACT.Identity, bias=nb0[:, t : t + 1], scale=a0[:, 1, t : t + 1]
-                    )
 
-        def regroup(c, g, lo, hi, on_scalar):
-            if g == 0:
-                src = xT[c // 4][:, :, (c % 4) * CH + lo : (c % 4) * CH + hi]
-            else:
-                src = xn[c][:, :, lo:hi]
-            src = src.rearrange("p t (c i) -> p c t i", i=4)
-            dst = gr[c][:, 4 * (g * CH + lo) : 4 * (g * CH + hi)].rearrange("p (c i t) -> p c t i", i=4, t=4)
-            if on_scalar:
-                nc.scalar.copy(out=dst, in_=src)
-            else:
-                nc.vector.tensor_copy(out=dst, in_=src)
+        def normalise_second(c):
+            xn[c] = gpool.tile([P, 4, CH], BF16, name="xn", tag="xn", align_bytes=64)
+            for t in range(4):
+                nc.scalar.activation(
+                    out=xn[c][:, t, :], in_=pts[c][t // 2][:, t % 2, :], func=ACT.Identity,
+                    bias=nb0[:, t : t + 1], scale=a0[:, 1, t : t + 1],
+                )
+
+        def regroup(c, g):
+            src = x_planes(c, 0, 4) if g == 0 else xn[c][:]
+            dst = gr[c][:, 4 * g * CH : 4 * (g + 1) * CH]
+            nc.vector.tensor_copy(
+                out=dst.rearrange("p (c i t) -> p c t i", i=4, t=4), in_=src.rearrange("p t (c i) -> p c t i", i=4)
+            )
 
         def quantise_x(c):
             nc.vector.quantize_mx(out=xq[c][:].bitcast(FP8X4), scales=xsc[c][:], in_=gr[c][:])
 
-        pts[0] = [x_transposed(0, 1, t) for t in range(4)]
+        pts[0] = [x_transposed(0, 1, u) for u in range(2)]
+        normalise_second(0)
         for i in range(NCH + 1):
+            if i + 1 < NCH:
+                pts[i + 1] = [x_transposed(i + 1, 1, u) for u in range(2)]
+                normalise_second(i + 1)
             if i < NCH:
                 gr[i] = gpool.tile([P, 8 * CH], BF16, name="gr", tag="gr", align_bytes=64)
-                xn[i] = gpool.tile([P, 4, CH], BF16, name="xn", tag="xn", align_bytes=64)
-                normalise_x(i)
-            if i == 0:
-                for m in range(MT):
-                    w_tile(m)
-            if i == 1:
-                for g in range(2):
-                    cols = slice(g * DOUT, (g + 1) * DOUT)
-                    nc.vector.quantize_mx(out=wq[:, cols].bitcast(FP8X4), scales=wsc[:, cols], in_=wg[:, g, :])
+                normalise_first(i)
             if i >= 1:
                 quantise_x(i - 1)
             if i < NCH:
-                cut = CH if i == 0 else (0 if i == 1 else 3 * CH // 4)
-                regroup(i, 0, 0, CH, False)
-                if cut > 0:
-                    regroup(i, 1, 0, cut, False)
-                if cut < CH:
-                    regroup(i, 1, cut, CH, True)
-            if i + 1 < NCH:
-                pts[i + 1] = [x_transposed(i + 1, 1, t) for t in range(4)]
+                regroup(i, 0)
+                regroup(i, 1)
             if i >= 1:
                 for m in range(NM2):
                     relu(m, i - 1, mx(m, i - 1))
@@ -328,12 +344,15 @@ def tile_settransform_pa_t_kernel(tc, set_feats, g0, b0, W0, c0, g1, b1, out):
             r1 = small.tile([P, 1], F32, name="r1", tag="r1")
             nc.vector.reciprocal(out=r1[:], in_=sd[:])
             a1 = small.tile([P, 2], F32, name="a1", tag="a1")
-            nc.vector.tensor_scalar(out=a1[:], in0=gpair[:, m, :], scalar1=r1[:, 0:1], scalar2=None, op0=ALU.mult)
-            d1 = small.tile([P, 1], F32, name="d1", tag="d1")
-            nc.vector.scalar_tensor_tensor(
-                out=d1[:], in0=mv[:, 0:1], scalar=a1[:, 1:2], in1=par[:, 32 + m : 33 + m], op0=ALU.mult, op1=ALU.add
+            nc.gpsimd.tensor_scalar(
+                out=a1[:], in0=gpair[:, m, :], scalar1=r1[:, 0:1], scalar2=1.0, op0=ALU.mult, op1=ALU.mult
             )
-            engines = "VVSV" if m == MT - 1 else "VGGG"
+            d1 = small.tile([P, 1], F32, name="d1", tag="d1")
+            nc.gpsimd.tensor_scalar(
+                out=d1[:], in0=mv[:, 0:1], scalar1=a1[:, 1:2], scalar2=par[:, 32 + m : 33 + m],
+                op0=ALU.mult, op1=ALU.add,
+            )
+            engines = "VVSV" if m == MT - 1 else "GGGG"
             for q in range(4):
                 hs = h[q, m // 4][:, :, m % 4, :]
                 if engines[q] == "S":
@@ -347,7 +366,10 @@ def tile_settransform_pa_t_kernel(tc, set_feats, g0, b0, W0, c0, g1, b1, out):
         def t_burst(m, half):
             banks = []
             for c in range(4 * half, 4 * half + 4):
-                pt = ps_t.tile([P, 4, P], F32, name="pto", tag="tp")
+                if c % 4 == 3:
+                    pt = ps_m.tile([P, 4, P], F32, name="ptm", tag="acc")
+                else:
+                    pt = ps_t.tile([P, 4, P], F32, name="pto", tag="tp")
                 banks.append(pt)
                 for jj in range(4):
                     nc.tensor.transpose(pt[:, jj, :], h_part(m, c)[:, jj, :], ident_f[:])
@@ -398,4 +420,4 @@ def tile_settransform_pa_t_kernel(tc, set_feats, g0, b0, W0, c0, g1, b1, out):
                 close_stats(mb)
             if banks:
                 evac(mt, 4 * th + 2, banks[2], False)
-                evac(mt, 4 * th + 3, banks[3], tail or th == 1)
+                evac(mt, 4 * th + 3, banks[3], True)

@@ -24,9 +24,16 @@ EPS = 1e-5
 FLOPS = 2 * ROWS * K * DOUT
 
 N_SUM = 16
+FULL = ()
+GRAM = tuple(c for c in range(NCH) if c not in FULL)
+W_AT = 8
+W_TILES = {100: (0, 1), 101: (1, 2), 102: (2, 4), 103: (4, 8)}
+W_V = ()
+WQ = 1
+SREG = 1
 NM2 = 5
-STORE_GROUPS = ((0, 1), (2, 3), (4, 5), (6,), (7,))
-LAG = 1
+STORE_GROUPS = ((0,), (1,), (2,), (3,), (4,), (5,), (6,), (7,))
+LAG = 2
 
 
 def tile_settransform_pa_t_kernel(tc, set_feats, g0, b0, W0, c0, g1, b1, out):
@@ -80,7 +87,10 @@ def tile_settransform_pa_t_kernel(tc, set_feats, g0, b0, W0, c0, g1, b1, out):
         nd0 = const.tile([P, 2, 4], F32, name="nd0")
         nb0 = const.tile([P, 4], F32, name="nb0")
         st1 = [const.tile([P, NCH, 6], F32, name="st1_%d" % m) for m in range(MT)]
+        stf = const.tile([P, 4, max(1, len(FULL)), 6], F32, name="stf")
+        mvf = const.tile([P, 4, 2], F32, name="mvf")
         h = {}
+        xn = {c: const.tile([P, 4, CH], BF16, name="xf%d" % c, align_bytes=64) for c in FULL}
 
         xs = [big.tile([P, 8, K], BF16, name="xs%d" % q, tag="hx", align_bytes=64) for q in range(4)]
         w_sb = big.tile([P, MT, K], BF16, name="w_sb", tag="ht", align_bytes=64)
@@ -91,10 +101,13 @@ def tile_settransform_pa_t_kernel(tc, set_feats, g0, b0, W0, c0, g1, b1, out):
 
         for i, v in enumerate((g0, b0, c0, g1, b1)):
             nc.scalar.dma_start(out=praw[2 * i : 2 * i + 2, :], in_=v.rearrange("(g f) -> g f", g=2))
-        for mp in range(4):
-            nc.sync.dma_start(out=w_sb[:, 2 * mp : 2 * mp + 2, :], in_=w_v[:, 2 * mp : 2 * mp + 2, :])
-        for c in range(NCH):
+        for c in range(NCH + 1):
             j0 = 4 * (c % 2)
+            if c == W_AT:
+                for mp in range(4):
+                    nc.sync.dma_start(out=w_sb[:, 2 * mp : 2 * mp + 2, :], in_=w_v[:, 2 * mp : 2 * mp + 2, :])
+            if c == NCH:
+                continue
             if c == 0:
                 for jj in range(4):
                     nc.sync.dma_start(out=xs[0][:, jj : jj + 1, :], in_=x_v[:, jj : jj + 1, :])
@@ -113,7 +126,9 @@ def tile_settransform_pa_t_kernel(tc, set_feats, g0, b0, W0, c0, g1, b1, out):
                 nc.tensor.transpose(pt[:, jj, :], x_rows(c, jj).bitcast(F32)[:, word_columns(g, u)], ident_f[:])
             return pt[:].rearrange("p j r -> p (j r)").bitcast(BF16).rearrange("p (r e) -> p e r", e=2)
 
-        def x_planes(c, t0, t1):
+        def x_planes(c, g, t0, t1):
+            if g == 1:
+                return xn[c][:, t0:t1, :]
             return xT[c // 4][:, t0:t1, (c % 4) * CH : (c % 4 + 1) * CH]
 
         def w_tile(m):
@@ -124,14 +139,12 @@ def tile_settransform_pa_t_kernel(tc, set_feats, g0, b0, W0, c0, g1, b1, out):
                     nc.tensor.transpose(pt[:, 2 * g + u, :], words[:, word_columns(g, u)], ident_f[:])
             dst = wg[:, :, 4 * m * P : 4 * (m + 1) * P].bitcast(F32).rearrange("p g (d u) -> p g d u", u=2)
             src = pt[:].rearrange("p (g u) d -> p g d u", u=2)
-            if m % 2 == 0:
-                nc.scalar.copy(out=dst, in_=src)
-            else:
+            if m in W_V:
                 nc.vector.tensor_copy(out=dst, in_=src)
+            else:
+                nc.scalar.copy(out=dst, in_=src)
 
-        for m in range(MT):
-            w_tile(m)
-        for g in range(2):
+        def quantise_w(g):
             cols = slice(g * DOUT, (g + 1) * DOUT)
             nc.vector.quantize_mx(out=wq[:, cols].bitcast(FP8X4), scales=wsc[:, cols], in_=wg[:, g, :])
 
@@ -148,14 +161,26 @@ def tile_settransform_pa_t_kernel(tc, set_feats, g0, b0, W0, c0, g1, b1, out):
         def scales_x(g):
             nc.vector.reciprocal(out=r0[:, g, :], in_=sd0[:, g, :])
             nc.vector.tensor_tensor(out=a0[:, g, :], in0=r0[:, g, :], in1=par_g[:, 0, g, :], op=ALU.mult)
-            nc.vector.tensor_tensor(out=ma0[:, g, :], in0=mv0[:, g, :, 0], in1=a0[:, g, :], op=ALU.mult)
+            mean = mv0[:, 0, :, 0] if g == 0 else tmp[:, 1, :]
+            nc.vector.tensor_tensor(out=ma0[:, g, :], in0=mean, in1=a0[:, g, :], op=ALU.mult)
             nc.vector.tensor_tensor(out=nd0[:, g, :], in0=ma0[:, g, :], in1=par_g[:, 1, g, :], op=ALU.subtract)
+
+        part = len(FULL) / NCH
+        e2f = const.tile([P, 4], F32, name="e2f")
+        tmp = const.tile([P, 2, 4], F32, name="tmp")
+
+        def full_sums():
+            for t in range(4):
+                nc.vector.bn_aggr(out=mvf[:, t, :], in_=stf[:, t, :, :].rearrange("p c s -> p (c s)"))
+            nc.vector.tensor_tensor(out=e2f[:], in0=mvf[:, :, 0], in1=mvf[:, :, 0], op=ALU.mult)
+            nc.vector.tensor_tensor(out=e2f[:], in0=e2f[:], in1=mvf[:, :, 1], op=ALU.add)
 
         def sorted_sums():
             pr = ps_t.tile([P, 4, 8], F32, name="pr", tag="tp")
             for t in range(4):
                 nc.tensor.matmul(
-                    out=pr[:, t, :], lhsT=sel[:, t, :], rhs=nat[:].rearrange("p s b -> p (s b)"), start=True, stop=True
+                    out=pr[:, t, :], lhsT=sel[:, t, :], rhs=nat[:].rearrange("p s b -> p (s b)"),
+                    start=True, stop=True,
                 )
             nc.vector.tensor_tensor(
                 out=srt[:], in0=pr[:].rearrange("p t (s b) -> p (t s) b", b=4), in1=quad[:], op=ALU.mult
@@ -164,14 +189,12 @@ def tile_settransform_pa_t_kernel(tc, set_feats, g0, b0, W0, c0, g1, b1, out):
                 out=raw[:].rearrange("p t s -> p (t s)"), in_=srt[:], axis=mybir.AxisListType.X, op=ALU.add
             )
             nc.vector.tensor_scalar(
-                out=mv0[:, 1, :, 0], in0=raw[:, :, 1], scalar1=1.0 / ROWS, scalar2=None, op0=ALU.mult
+                out=tmp[:].rearrange("p s t -> p t s"), in0=raw[:], scalar1=1.0 / ROWS, scalar2=None, op0=ALU.mult
             )
             ms = const.tile([P, 4], F32, name="ms")
-            nc.vector.tensor_tensor(out=ms[:], in0=mv0[:, 1, :, 0], in1=mv0[:, 1, :, 0], op=ALU.mult)
+            nc.vector.tensor_tensor(out=ms[:], in0=tmp[:, 1, :], in1=tmp[:, 1, :], op=ALU.mult)
             vr = const.tile([P, 4], F32, name="vr")
-            nc.vector.scalar_tensor_tensor(
-                out=vr[:], in0=raw[:, :, 0], scalar=1.0 / ROWS, in1=ms[:], op0=ALU.mult, op1=ALU.subtract
-            )
+            nc.vector.tensor_tensor(out=vr[:], in0=tmp[:, 0, :], in1=ms[:], op=ALU.subtract)
             nc.vector.tensor_scalar(out=mv0[:, 1, :, 1], in0=vr[:], scalar1=0.0, scalar2=None, op0=ALU.max)
 
         with tc.psum_pool(name="ps_g", bufs=1) as ps_g:
@@ -190,31 +213,35 @@ def tile_settransform_pa_t_kernel(tc, set_feats, g0, b0, W0, c0, g1, b1, out):
             def grams(c, b):
                 for jj in range(4):
                     x_b = x_rows(c, jj)[:, 512 + P * b : 512 + P * (b + 1)]
-                    first, last = c == 0 and jj == 0, c == NCH - 1 and jj == 3
+                    first, last = c == GRAM[0] and jj == 0, c == GRAM[-1] and jj == 3
                     nc.tensor.matmul(out=gram[b][:], lhsT=x_b, rhs=x_b, start=first, stop=last)
                     nc.tensor.matmul(
                         out=sums[:], lhsT=x_b, rhs=hot[:, b, :], start=first and b == 0, stop=last and b == 3
                     )
 
-            for c in range(NCH):
-                last = c == NCH - 1
-                if last:
-                    for b in range(4):
-                        grams(c, b)
-                for u in range(2):
-                    src = x_transposed(c, 0, u)
-                    nc.scalar.copy(out=x_planes(c, 2 * u, 2 * u + 2), in_=src)
-                    if not last:
-                        grams(c, 2 * u)
-                        grams(c, 2 * u + 1)
-                    elif u == 0:
-                        natural_sums()
-                    else:
-                        sorted_sums()
-                        deviation_x(1)
-                    for t in (2 * u, 2 * u + 1):
-                        nc.vector.bn_stats(out=st0[:, t, c, :], in_=x_planes(c, t, t + 1)[:, 0, :])
-                if c == 2:
+            def transposed_bank(c, g, u):
+                nc.scalar.copy(out=x_planes(c, g, 2 * u, 2 * u + 2), in_=x_transposed(c, g, u))
+
+            def bank_stats(c, g, u):
+                for t in (2 * u, 2 * u + 1):
+                    st = st0[:, t, c, :] if g == 0 else stf[:, t, FULL.index(c), :]
+                    nc.vector.bn_stats(out=st, in_=x_planes(c, g, t, t + 1)[:, 0, :])
+
+            banks = [(c, g, u) for c in range(NCH) for g in ((0, 1) if c in FULL else (0,)) for u in range(2)]
+            blocks = [(c, b) for c in GRAM for b in range(4)]
+            done = 0
+            for n, bank in enumerate(banks):
+                transposed_bank(*bank)
+                if n == len(banks) - 1:
+                    natural_sums()
+                bank_stats(*bank)
+                for m in range(*W_TILES.get(n, (0, 0))):
+                    w_tile(m)
+                target = min(len(blocks), len(blocks) * (n + 1) // (len(banks) - 1))
+                for block in blocks[done:target]:
+                    grams(*block)
+                done = target
+                if n == 6:
                     pps = ps_t.tile([P, 4, P], BF16, name="pps", tag="tp")
                     for t in range(4):
                         nc.tensor.transpose(pps[:, t, :], praw[:, t : t + 4 * (P - 1) + 1 : 4], ident_bf[:])
@@ -234,14 +261,24 @@ def tile_settransform_pa_t_kernel(tc, set_feats, g0, b0, W0, c0, g1, b1, out):
                         out=gpair[:, :, 1], in0=par[:, 24:32], scalar1=-1.0, scalar2=None, op0=ALU.mult
                     )
 
-        ps_m = ctx.enter_context(tc.psum_pool(name="ps_m", bufs=5))
+            for m in range(*W_TILES.get(100, (0, 0))):
+                w_tile(m)
+            sorted_sums()
+            for t in range(4):
+                nc.vector.bn_aggr(out=mv0[:, 0, t, :], in_=st0[:, t, :, :].rearrange("p c s -> p (c s)"))
+            for m in range(*W_TILES.get(101, (0, 0))):
+                w_tile(m)
+            deviation_x(1)
+            for m in range(*W_TILES.get(102, (0, 0))):
+                w_tile(m)
+            deviation_x(0)
 
-        for t in range(4):
-            nc.vector.bn_aggr(out=mv0[:, 0, t, :], in_=st0[:, t, :, :].rearrange("p c s -> p (c s)"))
+        for m in range(*W_TILES.get(103, (0, 0))):
+            w_tile(m)
         scales_x(1)
         nc.vector.tensor_scalar(out=nb0[:], in0=nd0[:, 1, :], scalar1=-1.0, scalar2=None, op0=ALU.mult)
-        deviation_x(0)
         scales_x(0)
+        ps_m = ctx.enter_context(tc.psum_pool(name="ps_m", bufs=5))
 
         def h_part(m, c):
             return h[c // 2, m // 4][:, 4 * (c % 2) : 4 * (c % 2) + 4, m % 4, :]
@@ -274,18 +311,18 @@ def tile_settransform_pa_t_kernel(tc, set_feats, g0, b0, W0, c0, g1, b1, out):
             nc.vector.bn_stats(out=st1[m][:, c, :], in_=h_part(m, c))
 
         gr = {}
-        xn = {}
         pts = {}
 
-        def normalise_first(c):
+        def normalise(c, g):
             for t in range(4):
-                plane = x_planes(c, t, t + 1)[:, 0, :]
+                plane = x_planes(c, g, t, t + 1)[:, 0, :]
                 nc.vector.tensor_scalar(
-                    out=plane, in0=plane, scalar1=a0[:, 0, t : t + 1], scalar2=nd0[:, 0, t : t + 1],
+                    out=plane, in0=plane, scalar1=a0[:, g, t : t + 1], scalar2=nd0[:, g, t : t + 1],
                     op0=ALU.mult, op1=ALU.subtract,
                 )
 
-        def normalise_second(c):
+        def transpose_late(c):
+            pts[c] = [x_transposed(c, 1, u) for u in range(2)]
             xn[c] = gpool.tile([P, 4, CH], BF16, name="xn", tag="xn", align_bytes=64)
             for t in range(4):
                 nc.scalar.activation(
@@ -293,30 +330,37 @@ def tile_settransform_pa_t_kernel(tc, set_feats, g0, b0, W0, c0, g1, b1, out):
                     bias=nb0[:, t : t + 1], scale=a0[:, 1, t : t + 1],
                 )
 
-        def regroup(c, g):
-            src = x_planes(c, 0, 4) if g == 0 else xn[c][:]
-            dst = gr[c][:, 4 * g * CH : 4 * (g + 1) * CH]
-            nc.vector.tensor_copy(
-                out=dst.rearrange("p (c i t) -> p c t i", i=4, t=4), in_=src.rearrange("p t (c i) -> p c t i", i=4)
-            )
+        def regroup(c, g, on_scalar):
+            src = x_planes(c, g, 0, 4).rearrange("p t (c i) -> p c t i", i=4)
+            dst = gr[c][:, 4 * g * CH : 4 * (g + 1) * CH].rearrange("p (c i t) -> p c t i", i=4, t=4)
+            if on_scalar:
+                nc.scalar.copy(out=dst, in_=src)
+            else:
+                nc.vector.tensor_copy(out=dst, in_=src)
 
         def quantise_x(c):
             nc.vector.quantize_mx(out=xq[c][:].bitcast(FP8X4), scales=xsc[c][:], in_=gr[c][:])
 
-        pts[0] = [x_transposed(0, 1, u) for u in range(2)]
-        normalise_second(0)
         for i in range(NCH + 1):
-            if i + 1 < NCH:
-                pts[i + 1] = [x_transposed(i + 1, 1, u) for u in range(2)]
-                normalise_second(i + 1)
+            if i == 0:
+                transpose_late(0)
+            if i > 0 and i + 1 < NCH:
+                transpose_late(i + 1)
             if i < NCH:
                 gr[i] = gpool.tile([P, 8 * CH], BF16, name="gr", tag="gr", align_bytes=64)
-                normalise_first(i)
+                normalise(i, 0)
+                if i in FULL:
+                    normalise(i, 1)
+            if i == WQ:
+                for g in range(2):
+                    quantise_w(g)
             if i >= 1:
                 quantise_x(i - 1)
             if i < NCH:
-                regroup(i, 0)
-                regroup(i, 1)
+                regroup(i, 0, False)
+                regroup(i, 1, i < SREG)
+            if i == 0:
+                transpose_late(1)
             if i >= 1:
                 for m in range(NM2):
                     relu(m, i - 1, mx(m, i - 1))
@@ -420,4 +464,4 @@ def tile_settransform_pa_t_kernel(tc, set_feats, g0, b0, W0, c0, g1, b1, out):
                 close_stats(mb)
             if banks:
                 evac(mt, 4 * th + 2, banks[2], False)
-                evac(mt, 4 * th + 3, banks[3], True)
+                evac(mt, 4 * th + 3, banks[3], tail or th == 1)

@@ -32,7 +32,7 @@ W_V = ()
 WQ = 1
 SREG = 1
 NM2 = 5
-STORE_GROUPS = ((0,), (1,), (2,), (3,), (4,), (5,), (6,), (7,))
+STORE_GROUPS = ((0, 1), (2, 3), (4, 5), (6, 7))
 LAG = 2
 
 

@@ -27,12 +27,17 @@ N_SUM = 16
 FULL = ()
 GRAM = tuple(c for c in range(NCH) if c not in FULL)
 W_AT = 8
-W_TILES = {100: (0, 1), 101: (1, 2), 102: (2, 4), 103: (4, 8)}
+W_TILES = {100: (0, 2), 101: (2, 4), 102: (4, 5), 103: (5, 8)}
 W_V = ()
 WQ = 1
 SREG = 1
-NM2 = 5
-STORE_GROUPS = ((0, 1), (2, 3), (4, 5), (6, 7))
+CUT = 512
+R_STEPS = 12
+LATE_W = (0,)
+LATE_V = (2,)
+SQ_TILES = ()
+NM2 = 6
+STORE_GROUPS = ((0,), (1,), (2,), (3,), (4,), (5,), (6,), (7,))
 LAG = 2
 
 
@@ -54,6 +59,8 @@ def tile_settransform_pa_t_kernel(tc, set_feats, g0, b0, W0, c0, g1, b1, out):
         warm = const.tile([P, 1], F32, name="warm")
         nc.scalar.activation(out=warm[:], in_=eps_t[:], func=ACT.Sqrt)
 
+        clk = const.tile([P, 2 * P], F32, name="clk")
+        nc.gpsimd.memset(clk[:], 1.0)
         praw = const.tile([P, 512], BF16, name="praw")
         nc.vector.memset(praw[:], 0.0)
         ident_f = const.tile([P, P], F32, name="ident_f")
@@ -87,6 +94,9 @@ def tile_settransform_pa_t_kernel(tc, set_feats, g0, b0, W0, c0, g1, b1, out):
         nd0 = const.tile([P, 2, 4], F32, name="nd0")
         nb0 = const.tile([P, 4], F32, name="nb0")
         st1 = [const.tile([P, NCH, 6], F32, name="st1_%d" % m) for m in range(MT)]
+        hsum = const.tile([P, MT, NCH], F32, name="hsum")
+        hsq = const.tile([P, MT, NCH], F32, name="hsq")
+        nmu1 = const.tile([P, MT], F32, name="nmu1")
         stf = const.tile([P, 4, max(1, len(FULL)), 6], F32, name="stf")
         mvf = const.tile([P, 4, 2], F32, name="mvf")
         h = {}
@@ -303,11 +313,28 @@ def tile_settransform_pa_t_kernel(tc, set_feats, g0, b0, W0, c0, g1, b1, out):
             return acc
 
         def relu(m, c, acc):
+            if m in SQ_TILES:
+                nc.scalar.activation(
+                    out=h_part(m, c), in_=acc[:], func=ACT.Relu, bias=par[:, 16 + m : 17 + m], scale=1.0,
+                    accum_out=hsum[:, m, c : c + 1],
+                )
+                return
             nc.scalar.activation(
                 out=h_part(m, c), in_=acc[:], func=ACT.Relu, bias=par[:, 16 + m : 17 + m], scale=1.0
             )
 
         def bn(m, c):
+            if m in SQ_TILES:
+                if c == 0:
+                    nc.scalar.activation(
+                        out=nmu1[:, m : m + 1], in_=hsum[:, m, 0:1], func=ACT.Copy, scale=-1.0 / CH
+                    )
+                junk = gpool.tile([P, 4, P], BF16, name="junk1", tag="junk1")
+                nc.scalar.activation(
+                    out=junk[:], in_=h_part(m, c), func=ACT.Square, bias=nmu1[:, m : m + 1], scale=1.0,
+                    accum_out=hsq[:, m, c : c + 1],
+                )
+                return
             nc.vector.bn_stats(out=st1[m][:, c, :], in_=h_part(m, c))
 
         gr = {}
@@ -321,18 +348,43 @@ def tile_settransform_pa_t_kernel(tc, set_feats, g0, b0, W0, c0, g1, b1, out):
                     op0=ALU.mult, op1=ALU.subtract,
                 )
 
-        def transpose_late(c):
-            pts[c] = [x_transposed(c, 1, u) for u in range(2)]
-            xn[c] = gpool.tile([P, 4, CH], BF16, name="xn", tag="xn", align_bytes=64)
-            for t in range(4):
-                nc.scalar.activation(
-                    out=xn[c][:, t, :], in_=pts[c][t // 2][:, t % 2, :], func=ACT.Identity,
-                    bias=nb0[:, t : t + 1], scale=a0[:, 1, t : t + 1],
-                )
+        todo = []
 
-        def regroup(c, g, on_scalar):
-            src = x_planes(c, g, 0, 4).rearrange("p t (c i) -> p c t i", i=4)
-            dst = gr[c][:, 4 * g * CH : 4 * (g + 1) * CH].rearrange("p (c i t) -> p c t i", i=4, t=4)
+        def late_v():
+            for c, t, src in todo:
+                nc.vector.tensor_scalar(
+                    out=xn[c][:, t, :], in0=src, scalar1=a0[:, 1, t : t + 1], scalar2=nd0[:, 1, t : t + 1],
+                    op0=ALU.mult, op1=ALU.subtract,
+                )
+            todo.clear()
+
+        def transpose_late(c):
+            xn[c] = gpool.tile([P, 4, CH], BF16, name="xn", tag="xn", align_bytes=64)
+            srcs = {}
+            for u in range(2):
+                if u in LATE_W:
+                    pt = x_transposed(c, 1, u)
+                    srcs[2 * u], srcs[2 * u + 1] = pt[:, 0, :], pt[:, 1, :]
+                else:
+                    for t in (2 * u, 2 * u + 1):
+                        ptl = ps_t.tile([P, 4, P], BF16, name="ptl", tag="tp")
+                        for jj in range(4):
+                            nc.tensor.transpose(ptl[:, jj, :], x_rows(c, jj)[:, 512 + t : 512 + t + 4 * (P - 1) + 1 : 4], ident_bf[:])
+                        srcs[t] = ptl[:].rearrange("p j r -> p (j r)")
+                for t in (2 * u, 2 * u + 1):
+                    if t in LATE_V:
+                        todo.append((c, t, srcs[t]))
+                    else:
+                        nc.scalar.activation(
+                            out=xn[c][:, t, :], in_=srcs[t], func=ACT.Identity, bias=nb0[:, t : t + 1],
+                            scale=a0[:, 1, t : t + 1],
+                        )
+
+        def regroup(c, g, lo, hi, on_scalar):
+            if lo == hi:
+                return
+            src = x_planes(c, g, 0, 4)[:, :, lo:hi].rearrange("p t (c i) -> p c t i", i=4)
+            dst = gr[c][:, 4 * (g * CH + lo) : 4 * (g * CH + hi)].rearrange("p (c i t) -> p c t i", i=4, t=4)
             if on_scalar:
                 nc.scalar.copy(out=dst, in_=src)
             else:
@@ -344,6 +396,7 @@ def tile_settransform_pa_t_kernel(tc, set_feats, g0, b0, W0, c0, g1, b1, out):
         for i in range(NCH + 1):
             if i == 0:
                 transpose_late(0)
+                late_v()
             if i > 0 and i + 1 < NCH:
                 transpose_late(i + 1)
             if i < NCH:
@@ -357,10 +410,13 @@ def tile_settransform_pa_t_kernel(tc, set_feats, g0, b0, W0, c0, g1, b1, out):
             if i >= 1:
                 quantise_x(i - 1)
             if i < NCH:
-                regroup(i, 0, False)
-                regroup(i, 1, i < SREG)
+                cut = 0 if i < SREG else CUT
+                regroup(i, 0, 0, CH, False)
+                regroup(i, 1, 0, cut, False)
+                regroup(i, 1, cut, CH, True)
             if i == 0:
                 transpose_late(1)
+            late_v()
             if i >= 1:
                 for m in range(NM2):
                     relu(m, i - 1, mx(m, i - 1))
@@ -374,6 +430,19 @@ def tile_settransform_pa_t_kernel(tc, set_feats, g0, b0, W0, c0, g1, b1, out):
 
         def close_stats(m):
             mv = small.tile([P, 2], F32, name="mv", tag="mv")
+            if m in SQ_TILES:
+                two = small.tile([P, 2], F32, name="two", tag="two")
+                nc.vector.tensor_reduce(out=two[:, 0:1], in_=hsum[:, m, :], axis=mybir.AxisListType.X, op=ALU.add)
+                nc.vector.tensor_reduce(out=two[:, 1:2], in_=hsq[:, m, :], axis=mybir.AxisListType.X, op=ALU.add)
+                nc.vector.tensor_scalar(out=mv[:, 0:1], in0=two[:, 0:1], scalar1=1.0 / ROWS, scalar2=None, op0=ALU.mult)
+                dd = small.tile([P, 2], F32, name="dd", tag="dd")
+                nc.vector.tensor_tensor(out=dd[:, 0:1], in0=mv[:, 0:1], in1=nmu1[:, m : m + 1], op=ALU.add)
+                nc.vector.tensor_tensor(out=dd[:, 1:2], in0=dd[:, 0:1], in1=dd[:, 0:1], op=ALU.mult)
+                nc.vector.scalar_tensor_tensor(
+                    out=mv[:, 1:2], in0=two[:, 1:2], scalar=1.0 / ROWS, in1=dd[:, 1:2], op0=ALU.mult, op1=ALU.subtract
+                )
+                stats[m] = mv
+                return
             nc.vector.bn_aggr(out=mv[:], in_=st1[m][:].rearrange("p c s -> p (c s)"))
             stats[m] = mv
 
@@ -407,6 +476,12 @@ def tile_settransform_pa_t_kernel(tc, set_feats, g0, b0, W0, c0, g1, b1, out):
                         out=hs, in0=hs, scalar1=a1[:, 0:1], scalar2=d1[:, 0:1], op0=ALU.mult, op1=ALU.add
                     )
 
+        def keep_clock():
+            pc = ps_m.tile([P, 4, P], F32, name="pc", tag="acc")
+            nc.tensor.matmul(
+                out=pc[:, 0:2, :].rearrange("p j r -> p (j r)"), lhsT=ident_f[:], rhs=clk[:], start=True, stop=True
+            )
+
         def t_burst(m, half):
             banks = []
             for c in range(4 * half, 4 * half + 4):
@@ -434,24 +509,29 @@ def tile_settransform_pa_t_kernel(tc, set_feats, g0, b0, W0, c0, g1, b1, out):
 
         close_stats(0)
         deviation(0)
-        n_late = 4 * (MT - NM2)
+        late = [(m, c) for m in range(NM2, MT) for c in range(NCH)]
+        n_done = 0
         for k in range(2 * MT + LAG):
             mb, hb = 1 + k // 2, k % 2
             chunks = range(4 * hb, 4 * hb + 4) if mb < MT else ()
             if k == 0:
                 chunks = range(2, 4)
             tail = mb >= MT
-            if k < n_late:
-                ml, cl = NM2 + k // 4, 2 * (k % 4)
-                accs = [mx(ml, cl + n) for n in range(2)]
-                for n in range(2):
-                    relu(ml, cl + n, accs[n])
+            target = min(len(late), -(-len(late) * (k + 1) // R_STEPS))
+            accs = [mx(*mc) for mc in late[n_done:target]]
+            for mc, acc in zip(late[n_done:target], accs):
+                relu(*mc, acc)
+            n_done = target
             banks = []
             if hb == 0 and 0 < k and mb <= MT:
                 deviation(mb - 1)
             if k >= LAG:
                 mt, th = (k - LAG) // 2, (k - LAG) % 2
+                if k >= R_STEPS:
+                    keep_clock()
                 banks = t_burst(mt, th)
+                if k >= R_STEPS:
+                    keep_clock()
                 evac(mt, 4 * th, banks[0], False)
                 evac(mt, 4 * th + 1, banks[1], tail)
             for c in chunks[:2]:

@@ -36,6 +36,10 @@ R_STEPS = 12
 LATE_W = (0,)
 LATE_V = (2,)
 SQ_TILES = ()
+KE = 192
+KL = 256
+V_SMALL = (7,)
+ENG = {7: "VVSV"}
 NM2 = 6
 STORE_GROUPS = ((0,), (1,), (2,), (3,), (4,), (5,), (6,), (7,))
 LAG = 2
@@ -457,15 +461,23 @@ def tile_settransform_pa_t_kernel(tc, set_feats, g0, b0, W0, c0, g1, b1, out):
             r1 = small.tile([P, 1], F32, name="r1", tag="r1")
             nc.vector.reciprocal(out=r1[:], in_=sd[:])
             a1 = small.tile([P, 2], F32, name="a1", tag="a1")
-            nc.gpsimd.tensor_scalar(
-                out=a1[:], in0=gpair[:, m, :], scalar1=r1[:, 0:1], scalar2=1.0, op0=ALU.mult, op1=ALU.mult
-            )
+            if m in V_SMALL:
+                nc.scalar.activation(out=a1[:], in_=gpair[:, m, :], func=ACT.Copy, scale=r1[:, 0:1])
+            else:
+                nc.gpsimd.tensor_scalar(
+                    out=a1[:], in0=gpair[:, m, :], scalar1=r1[:, 0:1], scalar2=1.0, op0=ALU.mult, op1=ALU.mult
+                )
             d1 = small.tile([P, 1], F32, name="d1", tag="d1")
-            nc.gpsimd.tensor_scalar(
-                out=d1[:], in0=mv[:, 0:1], scalar1=a1[:, 1:2], scalar2=par[:, 32 + m : 33 + m],
-                op0=ALU.mult, op1=ALU.add,
-            )
-            engines = "VVSV" if m == MT - 1 else "GGGG"
+            if m in V_SMALL:
+                nc.scalar.activation(
+                    out=d1[:], in_=mv[:, 0:1], func=ACT.Identity, bias=par[:, 32 + m : 33 + m], scale=a1[:, 1:2]
+                )
+            else:
+                nc.gpsimd.tensor_scalar(
+                    out=d1[:], in0=mv[:, 0:1], scalar1=a1[:, 1:2], scalar2=par[:, 32 + m : 33 + m],
+                    op0=ALU.mult, op1=ALU.add,
+                )
+            engines = ENG.get(m, "GGGG")
             for q in range(4):
                 hs = h[q, m // 4][:, :, m % 4, :]
                 if engines[q] == "S":
@@ -476,15 +488,19 @@ def tile_settransform_pa_t_kernel(tc, set_feats, g0, b0, W0, c0, g1, b1, out):
                         out=hs, in0=hs, scalar1=a1[:, 0:1], scalar2=d1[:, 0:1], op0=ALU.mult, op1=ALU.add
                     )
 
-        def keep_clock():
+        def keep_clock(n):
+            if n == 0:
+                return
             pc = ps_m.tile([P, 4, P], F32, name="pc", tag="acc")
             nc.tensor.matmul(
-                out=pc[:, 0:2, :].rearrange("p j r -> p (j r)"), lhsT=ident_f[:], rhs=clk[:], start=True, stop=True
+                out=pc[:].rearrange("p j r -> p (j r)")[:, 0:n], lhsT=ident_f[:], rhs=clk[:, 0:n], start=True, stop=True
             )
 
-        def t_burst(m, half):
+        def t_burst(m, half, n):
             banks = []
             for c in range(4 * half, 4 * half + 4):
+                if c % 2 == 0:
+                    keep_clock(n)
                 if c % 4 == 3:
                     pt = ps_m.tile([P, 4, P], F32, name="ptm", tag="acc")
                 else:
@@ -527,11 +543,7 @@ def tile_settransform_pa_t_kernel(tc, set_feats, g0, b0, W0, c0, g1, b1, out):
                 deviation(mb - 1)
             if k >= LAG:
                 mt, th = (k - LAG) // 2, (k - LAG) % 2
-                if k >= R_STEPS:
-                    keep_clock()
-                banks = t_burst(mt, th)
-                if k >= R_STEPS:
-                    keep_clock()
+                banks = t_burst(mt, th, KL if k >= R_STEPS else KE)
                 evac(mt, 4 * th, banks[0], False)
                 evac(mt, 4 * th + 1, banks[1], tail)
             for c in chunks[:2]:

from contextlib import ExitStack

import concourse.mybir as mybir
from concourse.masks import make_identity

F32 = mybir.dt.float32
BF16 = mybir.dt.bfloat16
U32 = mybir.dt.uint32
U8 = mybir.dt.uint8
FP8X4 = mybir.dt.float8_e4m3fn_x4
ACT = mybir.ActivationFunctionType
ALU = mybir.AluOpType

P = 128
ROWS = 4096
K = 1024
DOUT = 1024
RT = ROWS // P
KB = K // P
MT = DOUT // P
CH = 512
NCH = ROWS // CH
EPS = 1e-5
FLOPS = 2 * ROWS * K * DOUT

N_SUM = 16
FULL = ()
GRAM = tuple(c for c in range(NCH) if c not in FULL)
W_AT = 8
W_TILES = {100: (0, 2), 101: (2, 4), 102: (4, 5), 103: (5, 8)}
W_V = ()
WQ = 1
SREG = 1
CUT = 512
R_STEPS = 12
LATE_W = (0,)
LATE_V = (2,)
SQ_TILES = ()
KE = 192
KL = 256
V_SMALL = (7,)
ENG = {7: "VVSV"}
NM2 = 6
STORE_GROUPS = ((0,), (1,), (2,), (3,), (4,), (5,), (6,), (7,))
LAG = 2


def tile_settransform_pa_t_kernel(tc, set_feats, g0, b0, W0, c0, g1, b1, out):
    nc = tc.nc
    x_v = set_feats.flatten_outer_dims().rearrange("(p j) k -> p j k", j=RT)
    out_v = out.flatten_outer_dims().rearrange("(p j) d -> p j d", j=RT)
    w_v = W0.rearrange("(m p) k -> p m k", p=P)

    with ExitStack() as ctx:
        const = ctx.enter_context(tc.tile_pool(name="const", bufs=1))
        big = ctx.enter_context(tc.tile_pool(name="big", bufs=4))
        gpool = ctx.enter_context(tc.tile_pool(name="gpool", bufs=3))
        small = ctx.enter_context(tc.tile_pool(name="small", bufs=3))
        ps_t = ctx.enter_context(tc.psum_pool(name="ps_t", bufs=3))

        eps_t = const.tile([P, 1], F32, name="eps_t")
        nc.vector.memset(eps_t[:], EPS)
        warm = const.tile([P, 1], F32, name="warm")
        nc.scalar.activation(out=warm[:], in_=eps_t[:], func=ACT.Sqrt)

        clk = const.tile([P, 2 * P], F32, name="clk")
        nc.gpsimd.memset(clk[:], 1.0)
        praw = const.tile([P, 512], BF16, name="praw")
        nc.vector.memset(praw[:], 0.0)
        ident_f = const.tile([P, P], F32, name="ident_f")
        make_identity(nc, ident_f[:])
        ident_bf = const.tile([P, P], BF16, name="ident_bf")
        nc.vector.tensor_copy(out=ident_bf[:], in_=ident_f[:])
        hot = const.tile([P, 4, N_SUM], BF16, name="hot")
        nc.vector.memset(hot[:], 0.0)
        for b in range(4):
            nc.vector.memset(hot[:, b, b : b + 1], 1.0)
        sel = const.tile([P, 4, P], F32, name="sel")
        quad = const.tile([P, 8, 4], F32, name="quad")
        nc.vector.memset(quad[:], 0.0)
        for b in range(4):
            nc.vector.memset(quad[32 * b : 32 * b + 32, :, b : b + 1], 1.0)
            for t in range(4):
                nc.vector.tensor_copy(out=sel[:, t, 32 * b : 32 * b + 32], in_=ident_f[:, t : t + 125 : 4])

        par = const.tile([P, 40], F32, name="par")
        gpair = const.tile([P, MT, 2], F32, name="gpair")
        xq = [const.tile([P, 2 * CH], U32, name="xq%d" % c, align_bytes=64) for c in range(NCH)]
        xsc = [const.tile([P, 2 * CH], U8, name="xsc%d" % c, align_bytes=64) for c in range(NCH)]
        wq = const.tile([P, 2 * DOUT], U32, name="wq", align_bytes=64)
        wsc = const.tile([P, 2 * DOUT], U8, name="wsc", align_bytes=64)
        st0 = const.tile([P, 4, NCH, 6], F32, name="st0")
        mv0 = const.tile([P, 2, 4, 2], F32, name="mv0")
        nat = const.tile([P, 2, 4], F32, name="nat")
        srt = const.tile([P, 8, 4], F32, name="srt")
        raw = const.tile([P, 4, 2], F32, name="raw")
        a0 = const.tile([P, 2, 4], F32, name="a0")
        nd0 = const.tile([P, 2, 4], F32, name="nd0")
        nb0 = const.tile([P, 4], F32, name="nb0")
        st1 = [const.tile([P, NCH, 6], F32, name="st1_%d" % m) for m in range(MT)]
        hsum = const.tile([P, MT, NCH], F32, name="hsum")
        hsq = const.tile([P, MT, NCH], F32, name="hsq")
        nmu1 = const.tile([P, MT], F32, name="nmu1")
        stf = const.tile([P, 4, max(1, len(FULL)), 6], F32, name="stf")
        mvf = const.tile([P, 4, 2], F32, name="mvf")
        h = {}
        xn = {c: const.tile([P, 4, CH], BF16, name="xf%d" % c, align_bytes=64) for c in FULL}

        xs = [big.tile([P, 8, K], BF16, name="xs%d" % q, tag="hx", align_bytes=64) for q in range(4)]
        w_sb = big.tile([P, MT, K], BF16, name="w_sb", tag="ht", align_bytes=64)
        wg = big.tile([P, 2, 4 * DOUT], BF16, name="wg", tag="ht", align_bytes=64)
        xT = [big.tile([P, 4, 4 * CH], BF16, name="xT%d" % q, tag="ht", align_bytes=64) for q in range(2)]

        ctx.enter_context(tc.manual_schedule())

        for i, v in enumerate((g0, b0, c0, g1, b1)):
            nc.scalar.dma_start(out=praw[2 * i : 2 * i + 2, :], in_=v.rearrange("(g f) -> g f", g=2))
        for c in range(NCH + 1):
            j0 = 4 * (c % 2)
            if c == W_AT:
                for mp in range(4):
                    nc.sync.dma_start(out=w_sb[:, 2 * mp : 2 * mp + 2, :], in_=w_v[:, 2 * mp : 2 * mp + 2, :])
            if c == NCH:
                continue
            if c == 0:
                for jj in range(4):
                    nc.sync.dma_start(out=xs[0][:, jj : jj + 1, :], in_=x_v[:, jj : jj + 1, :])
            else:
                nc.sync.dma_start(out=xs[c // 2][:, j0 : j0 + 4, :], in_=x_v[:, 4 * c : 4 * c + 4, :])

        def x_rows(c, jj):
            return xs[c // 2][:, 4 * (c % 2) + jj, :]

        def word_columns(g, u):
            return slice(256 * g + u, 256 * g + u + 2 * (P - 1) + 1, 2)

        def x_transposed(c, g, u):
            pt = ps_t.tile([P, 4, P], F32, name="pt", tag="tp")
            for jj in range(4):
                nc.tensor.transpose(pt[:, jj, :], x_rows(c, jj).bitcast(F32)[:, word_columns(g, u)], ident_f[:])
            return pt[:].rearrange("p j r -> p (j r)").bitcast(BF16).rearrange("p (r e) -> p e r", e=2)

        def x_planes(c, g, t0, t1):
            if g == 1:
                return xn[c][:, t0:t1, :]
            return xT[c // 4][:, t0:t1, (c % 4) * CH : (c % 4 + 1) * CH]

        def w_tile(m):
            words = w_sb[:, m, :].bitcast(F32)
            pt = ps_t.tile([P, 4, P], F32, name="ptw", tag="tp")
            for g in range(2):
                for u in range(2):
                    nc.tensor.transpose(pt[:, 2 * g + u, :], words[:, word_columns(g, u)], ident_f[:])
            dst = wg[:, :, 4 * m * P : 4 * (m + 1) * P].bitcast(F32).rearrange("p g (d u) -> p g d u", u=2)
            src = pt[:].rearrange("p (g u) d -> p g d u", u=2)
            if m in W_V:
                nc.vector.tensor_copy(out=dst, in_=src)
            else:
                nc.scalar.copy(out=dst, in_=src)

        def quantise_w(g):
            cols = slice(g * DOUT, (g + 1) * DOUT)
            nc.vector.quantize_mx(out=wq[:, cols].bitcast(FP8X4), scales=wsc[:, cols], in_=wg[:, g, :])

        sd0 = const.tile([P, 2, 4], F32, name="sd0")
        r0 = const.tile([P, 2, 4], F32, name="r0")
        ma0 = const.tile([P, 2, 4], F32, name="ma0")
        par_g = par[:, 0:16].rearrange("p (v g t) -> p v g t", v=2, g=2)

        def deviation_x(g):
            nc.scalar.activation(
                out=sd0[:, g, :], in_=mv0[:, g, :, 1], func=ACT.Sqrt, bias=eps_t[:, 0:1], scale=1.0
            )

        def scales_x(g):
            nc.vector.reciprocal(out=r0[:, g, :], in_=sd0[:, g, :])
            nc.vector.tensor_tensor(out=a0[:, g, :], in0=r0[:, g, :], in1=par_g[:, 0, g, :], op=ALU.mult)
            mean = mv0[:, 0, :, 0] if g == 0 else tmp[:, 1, :]
            nc.vector.tensor_tensor(out=ma0[:, g, :], in0=mean, in1=a0[:, g, :], op=ALU.mult)
            nc.vector.tensor_tensor(out=nd0[:, g, :], in0=ma0[:, g, :], in1=par_g[:, 1, g, :], op=ALU.subtract)

        part = len(FULL) / NCH
        e2f = const.tile([P, 4], F32, name="e2f")
        tmp = const.tile([P, 2, 4], F32, name="tmp")

        def full_sums():
            for t in range(4):
                nc.vector.bn_aggr(out=mvf[:, t, :], in_=stf[:, t, :, :].rearrange("p c s -> p (c s)"))
            nc.vector.tensor_tensor(out=e2f[:], in0=mvf[:, :, 0], in1=mvf[:, :, 0], op=ALU.mult)
            nc.vector.tensor_tensor(out=e2f[:], in0=e2f[:], in1=mvf[:, :, 1], op=ALU.add)

        def sorted_sums():
            pr = ps_t.tile([P, 4, 8], F32, name="pr", tag="tp")
            for t in range(4):
                nc.tensor.matmul(
                    out=pr[:, t, :], lhsT=sel[:, t, :], rhs=nat[:].rearrange("p s b -> p (s b)"),
                    start=True, stop=True,
                )
            nc.vector.tensor_tensor(
                out=srt[:], in0=pr[:].rearrange("p t (s b) -> p (t s) b", b=4), in1=quad[:], op=ALU.mult
            )
            nc.vector.tensor_reduce(
                out=raw[:].rearrange("p t s -> p (t s)"), in_=srt[:], axis=mybir.AxisListType.X, op=ALU.add
            )
            nc.vector.tensor_scalar(
                out=tmp[:].rearrange("p s t -> p t s"), in0=raw[:], scalar1=1.0 / ROWS, scalar2=None, op0=ALU.mult
            )
            ms = const.tile([P, 4], F32, name="ms")
            nc.vector.tensor_tensor(out=ms[:], in0=tmp[:, 1, :], in1=tmp[:, 1, :], op=ALU.mult)
            vr = const.tile([P, 4], F32, name="vr")
            nc.vector.tensor_tensor(out=vr[:], in0=tmp[:, 0, :], in1=ms[:], op=ALU.subtract)
            nc.vector.tensor_scalar(out=mv0[:, 1, :, 1], in0=vr[:], scalar1=0.0, scalar2=None, op0=ALU.max)

        with tc.psum_pool(name="ps_g", bufs=1) as ps_g:
            gram = [ps_g.tile([P, P], F32, name="gram%d" % b) for b in range(4)]
            sums = ps_g.tile([P, N_SUM], F32, name="sums")

            def natural_sums():
                for b in range(4):
                    junk = gpool.tile([P, P], F32, name="junk", tag="junk")
                    nc.vector.scalar_tensor_tensor(
                        out=junk[:], in0=gram[b][:], scalar=1.0, in1=ident_f[:],
                        op0=ALU.mult, op1=ALU.mult, accum_out=nat[:, 0, b : b + 1],
                    )
                nc.vector.tensor_copy(out=nat[:, 1, :], in_=sums[:, 0:4])

            def grams(c, b):
                for jj in range(4):
                    x_b = x_rows(c, jj)[:, 512 + P * b : 512 + P * (b + 1)]
                    first, last = c == GRAM[0] and jj == 0, c == GRAM[-1] and jj == 3
                    nc.tensor.matmul(out=gram[b][:], lhsT=x_b, rhs=x_b, start=first, stop=last)
                    nc.tensor.matmul(
                        out=sums[:], lhsT=x_b, rhs=hot[:, b, :], start=first and b == 0, stop=last and b == 3
                    )

            def transposed_bank(c, g, u):
                nc.scalar.copy(out=x_planes(c, g, 2 * u, 2 * u + 2), in_=x_transposed(c, g, u))

            def bank_stats(c, g, u):
                for t in (2 * u, 2 * u + 1):
                    st = st0[:, t, c, :] if g == 0 else stf[:, t, FULL.index(c), :]
                    nc.vector.bn_stats(out=st, in_=x_planes(c, g, t, t + 1)[:, 0, :])

            banks = [(c, g, u) for c in range(NCH) for g in ((0, 1) if c in FULL else (0,)) for u in range(2)]
            blocks = [(c, b) for c in GRAM for b in range(4)]
            done = 0
            for n, bank in enumerate(banks):
                transposed_bank(*bank)
                if n == len(banks) - 1:
                    natural_sums()
                bank_stats(*bank)
                for m in range(*W_TILES.get(n, (0, 0))):
                    w_tile(m)
                target = min(len(blocks), len(blocks) * (n + 1) // (len(banks) - 1))
                for block in blocks[done:target]:
                    grams(*block)
                done = target
                if n == 6:
                    pps = ps_t.tile([P, 4, P], BF16, name="pps", tag="tp")
                    for t in range(4):
                        nc.tensor.transpose(pps[:, t, :], praw[:, t : t + 4 * (P - 1) + 1 : 4], ident_bf[:])
                    nc.vector.tensor_copy(
                        out=par[:, 0:16].rearrange("p (r t) -> p r t", t=4),
                        in_=pps[:, :, 0:4].rearrange("p t r -> p r t"),
                    )
                    ppo = ps_t.tile([P, 4, P], BF16, name="ppo", tag="tp")
                    for j in range(4):
                        nc.tensor.transpose(ppo[:, j, :], praw[:, j * P : (j + 1) * P], ident_bf[:])
                    nc.vector.tensor_copy(
                        out=par[:, 16:40].rearrange("p (r j) -> p r j", j=4),
                        in_=ppo[:, :, 4:10].rearrange("p j r -> p r j"),
                    )
                    nc.vector.tensor_copy(out=gpair[:, :, 0], in_=par[:, 24:32])
                    nc.vector.tensor_scalar(
                        out=gpair[:, :, 1], in0=par[:, 24:32], scalar1=-1.0, scalar2=None, op0=ALU.mult
                    )

            for m in range(*W_TILES.get(100, (0, 0))):
                w_tile(m)
            sorted_sums()
            for t in range(4):
                nc.vector.bn_aggr(out=mv0[:, 0, t, :], in_=st0[:, t, :, :].rearrange("p c s -> p (c s)"))
            for m in range(*W_TILES.get(101, (0, 0))):
                w_tile(m)
            deviation_x(1)
            for m in range(*W_TILES.get(102, (0, 0))):
                w_tile(m)
            deviation_x(0)

        for m in range(*W_TILES.get(103, (0, 0))):
            w_tile(m)
        scales_x(1)
        nc.vector.tensor_scalar(out=nb0[:], in0=nd0[:, 1, :], scalar1=-1.0, scalar2=None, op0=ALU.mult)
        scales_x(0)
        ps_m = ctx.enter_context(tc.psum_pool(name="ps_m", bufs=5))

        def h_part(m, c):
            return h[c // 2, m // 4][:, 4 * (c % 2) : 4 * (c % 2) + 4, m % 4, :]

        def mx(m, c):
            key = (c // 2, m // 4)
            if key not in h:
                tag = "hx" if key[1] == 0 else "ht"
                h[key] = big.tile([P, 8, 4, P], F32, name="h%d_%d" % key, tag=tag, align_bytes=64)
            acc = ps_m.tile([P, 4, P], F32, name="acc", tag="acc")
            for g in range(2):
                lo = g * DOUT + m * P
                nc.tensor.matmul_mx(
                    out=acc[:].rearrange("p j r -> p (j r)"),
                    lhsT=wq[:, lo : lo + P].bitcast(FP8X4),
                    lhsT_scale=wsc[:, lo : lo + P],
                    rhs=xq[c][:, g * CH : (g + 1) * CH].bitcast(FP8X4),
                    rhs_scale=xsc[c][:, g * CH : (g + 1) * CH],
                    start=(g == 0),
                    stop=(g == 1),
                )
            return acc

        def relu(m, c, acc):
            if m in SQ_TILES:
                nc.scalar.activation(
                    out=h_part(m, c), in_=acc[:], func=ACT.Relu, bias=par[:, 16 + m : 17 + m], scale=1.0,
                    accum_out=hsum[:, m, c : c + 1],
                )
                return
            nc.scalar.activation(
                out=h_part(m, c), in_=acc[:], func=ACT.Relu, bias=par[:, 16 + m : 17 + m], scale=1.0
            )

        def bn(m, c):
            if m in SQ_TILES:
                if c == 0:
                    nc.scalar.activation(
                        out=nmu1[:, m : m + 1], in_=hsum[:, m, 0:1], func=ACT.Copy, scale=-1.0 / CH
                    )
                junk = gpool.tile([P, 4, P], BF16, name="junk1", tag="junk1")
                nc.scalar.activation(
                    out=junk[:], in_=h_part(m, c), func=ACT.Square, bias=nmu1[:, m : m + 1], scale=1.0,
                    accum_out=hsq[:, m, c : c + 1],
                )
                return
            nc.vector.bn_stats(out=st1[m][:, c, :], in_=h_part(m, c))

        gr = {}
        pts = {}

        def normalise(c, g):
            for t in range(4):
                plane = x_planes(c, g, t, t + 1)[:, 0, :]
                nc.vector.tensor_scalar(
                    out=plane, in0=plane, scalar1=a0[:, g, t : t + 1], scalar2=nd0[:, g, t : t + 1],
                    op0=ALU.mult, op1=ALU.subtract,
                )

        todo = []

        def late_v():
            for c, t, src in todo:
                nc.vector.tensor_scalar(
                    out=xn[c][:, t, :], in0=src, scalar1=a0[:, 1, t : t + 1], scalar2=nd0[:, 1, t : t + 1],
                    op0=ALU.mult, op1=ALU.subtract,
                )
            todo.clear()

        def transpose_late(c):
            xn[c] = gpool.tile([P, 4, CH], BF16, name="xn", tag="xn", align_bytes=64)
            srcs = {}
            for u in range(2):
                if u in LATE_W:
                    pt = x_transposed(c, 1, u)
                    srcs[2 * u], srcs[2 * u + 1] = pt[:, 0, :], pt[:, 1, :]
                else:
                    for t in (2 * u, 2 * u + 1):
                        ptl = ps_t.tile([P, 4, P], BF16, name="ptl", tag="tp")
                        for jj in range(4):
                            nc.tensor.transpose(ptl[:, jj, :], x_rows(c, jj)[:, 512 + t : 512 + t + 4 * (P - 1) + 1 : 4], ident_bf[:])
                        srcs[t] = ptl[:].rearrange("p j r -> p (j r)")
                for t in (2 * u, 2 * u + 1):
                    if t in LATE_V:
                        todo.append((c, t, srcs[t]))
                    else:
                        nc.scalar.activation(
                            out=xn[c][:, t, :], in_=srcs[t], func=ACT.Identity, bias=nb0[:, t : t + 1],
                            scale=a0[:, 1, t : t + 1],
                        )

        def regroup(c, g, lo, hi, on_scalar):
            if lo == hi:
                return
            src = x_planes(c, g, 0, 4)[:, :, lo:hi].rearrange("p t (c i) -> p c t i", i=4)
            dst = gr[c][:, 4 * (g * CH + lo) : 4 * (g * CH + hi)].rearrange("p (c i t) -> p c t i", i=4, t=4)
            if on_scalar:
                nc.scalar.copy(out=dst, in_=src)
            else:
                nc.vector.tensor_copy(out=dst, in_=src)

        def quantise_x(c):
            nc.vector.quantize_mx(out=xq[c][:].bitcast(FP8X4), scales=xsc[c][:], in_=gr[c][:])

        for i in range(NCH + 1):
            if i == 0:
                transpose_late(0)
                late_v()
            if i > 0 and i + 1 < NCH:
                transpose_late(i + 1)
            if i < NCH:
                gr[i] = gpool.tile([P, 8 * CH], BF16, name="gr", tag="gr", align_bytes=64)
                normalise(i, 0)
                if i in FULL:
                    normalise(i, 1)
            if i == WQ:
                for g in range(2):
                    quantise_w(g)
            if i >= 1:
                quantise_x(i - 1)
            if i < NCH:
                cut = 0 if i < SREG else CUT
                regroup(i, 0, 0, CH, False)
                regroup(i, 1, 0, cut, False)
                regroup(i, 1, cut, CH, True)
            if i == 0:
                transpose_late(1)
            late_v()
            if i >= 1:
                for m in range(NM2):
                    relu(m, i - 1, mx(m, i - 1))
            if 2 <= i <= NCH:
                bn(0, i - 2)
        for c in range(2):
            bn(1, c)
        bn(0, NCH - 1)

        stats = {}

        def close_stats(m):
            mv = small.tile([P, 2], F32, name="mv", tag="mv")
            if m in SQ_TILES:
                two = small.tile([P, 2], F32, name="two", tag="two")
                nc.vector.tensor_reduce(out=two[:, 0:1], in_=hsum[:, m, :], axis=mybir.AxisListType.X, op=ALU.add)
                nc.vector.tensor_reduce(out=two[:, 1:2], in_=hsq[:, m, :], axis=mybir.AxisListType.X, op=ALU.add)
                nc.vector.tensor_scalar(out=mv[:, 0:1], in0=two[:, 0:1], scalar1=1.0 / ROWS, scalar2=None, op0=ALU.mult)
                dd = small.tile([P, 2], F32, name="dd", tag="dd")
                nc.vector.tensor_tensor(out=dd[:, 0:1], in0=mv[:, 0:1], in1=nmu1[:, m : m + 1], op=ALU.add)
                nc.vector.tensor_tensor(out=dd[:, 1:2], in0=dd[:, 0:1], in1=dd[:, 0:1], op=ALU.mult)
                nc.vector.scalar_tensor_tensor(
                    out=mv[:, 1:2], in0=two[:, 1:2], scalar=1.0 / ROWS, in1=dd[:, 1:2], op0=ALU.mult, op1=ALU.subtract
                )
                stats[m] = mv
                return
            nc.vector.bn_aggr(out=mv[:], in_=st1[m][:].rearrange("p c s -> p (c s)"))
            stats[m] = mv

        def deviation(m):
            mv = stats[m]
            sd = small.tile([P, 1], F32, name="sd", tag="sd")
            nc.scalar.activation(out=sd[:], in_=mv[:, 1:2], func=ACT.Sqrt, bias=eps_t[:, 0:1], scale=1.0)
            stats[m] = (mv, sd)

        def norm_out(m):
            mv, sd = stats[m]
            r1 = small.tile([P, 1], F32, name="r1", tag="r1")
            nc.vector.reciprocal(out=r1[:], in_=sd[:])
            a1 = small.tile([P, 2], F32, name="a1", tag="a1")
            if m in V_SMALL:
                nc.scalar.activation(out=a1[:], in_=gpair[:, m, :], func=ACT.Copy, scale=r1[:, 0:1])
            else:
                nc.gpsimd.tensor_scalar(
                    out=a1[:], in0=gpair[:, m, :], scalar1=r1[:, 0:1], scalar2=1.0, op0=ALU.mult, op1=ALU.mult
                )
            d1 = small.tile([P, 1], F32, name="d1", tag="d1")
            if m in V_SMALL:
                nc.scalar.activation(
                    out=d1[:], in_=mv[:, 0:1], func=ACT.Identity, bias=par[:, 32 + m : 33 + m], scale=a1[:, 1:2]
                )
            else:
                nc.gpsimd.tensor_scalar(
                    out=d1[:], in0=mv[:, 0:1], scalar1=a1[:, 1:2], scalar2=par[:, 32 + m : 33 + m],
                    op0=ALU.mult, op1=ALU.add,
                )
            engines = ENG.get(m, "GGGG")
            for q in range(4):
                hs = h[q, m // 4][:, :, m % 4, :]
                if engines[q] == "S":
                    nc.scalar.activation(out=hs, in_=hs, func=ACT.Identity, bias=d1[:, 0:1], scale=a1[:, 0:1])
                else:
                    eng = nc.vector if engines[q] == "V" else nc.gpsimd
                    eng.tensor_scalar(
                        out=hs, in0=hs, scalar1=a1[:, 0:1], scalar2=d1[:, 0:1], op0=ALU.mult, op1=ALU.add
                    )

        def keep_clock(n):
            if n == 0:
                return
            pc = ps_m.tile([P, 4, P], F32, name="pc", tag="acc")
            nc.tensor.matmul(
                out=pc[:].rearrange("p j r -> p (j r)")[:, 0:n], lhsT=ident_f[:], rhs=clk[:, 0:n], start=True, stop=True
            )

        def t_burst(m, half, n):
            banks = []
            for c in range(4 * half, 4 * half + 4):
                if c % 2 == 0:
                    keep_clock(n)
                if c % 4 == 3:
                    pt = ps_m.tile([P, 4, P], F32, name="ptm", tag="acc")
                else:
                    pt = ps_t.tile([P, 4, P], F32, name="pto", tag="tp")
                banks.append(pt)
                for jj in range(4):
                    nc.tensor.transpose(pt[:, jj, :], h_part(m, c)[:, jj, :], ident_f[:])
            return banks

        def evac(m, c, pt, on_vector):
            if on_vector:
                nc.vector.tensor_copy(out=h_part(m, c), in_=pt[:])
            else:
                nc.scalar.copy(out=h_part(m, c), in_=pt[:])
            grp = [gr_ for gr_ in STORE_GROUPS if m in gr_][0]
            if m == grp[-1] and c % 2 == 1:
                q = c // 2
                nc.sync.dma_start(
                    out=out_v[:, 8 * q : 8 * q + 8, grp[0] * P : (m + 1) * P],
                    in_=h[q, m // 4][:, :, grp[0] % 4 : m % 4 + 1, :].rearrange("p j m f -> p j (m f)"),
                )

        close_stats(0)
        deviation(0)
        late = [(m, c) for m in range(NM2, MT) for c in range(NCH)]
        n_done = 0
        for k in range(2 * MT + LAG):
            mb, hb = 1 + k // 2, k % 2
            chunks = range(4 * hb, 4 * hb + 4) if mb < MT else ()
            if k == 0:
                chunks = range(2, 4)
            tail = mb >= MT
            target = min(len(late), -(-len(late) * (k + 1) // R_STEPS))
            accs = [mx(*mc) for mc in late[n_done:target]]
            for mc, acc in zip(late[n_done:target], accs):
                relu(*mc, acc)
            n_done = target
            banks = []
            if hb == 0 and 0 < k and mb <= MT:
                deviation(mb - 1)
            if k >= LAG:
                mt, th = (k - LAG) // 2, (k - LAG) % 2
                banks = t_burst(mt, th, KL if k >= R_STEPS else KE)
                evac(mt, 4 * th, banks[0], False)
                evac(mt, 4 * th + 1, banks[1], tail)
            for c in chunks[:2]:
                bn(mb, c)
            if hb == 0 and mb <= MT:
                norm_out(mb - 1)
            for c in chunks[2:]:
                bn(mb, c)
            if chunks and hb == 1:
                close_stats(mb)
            if banks:
                evac(mt, 4 * th + 2, banks[2], False)
                evac(mt, 4 * th + 3, banks[3], tail or th == 1)
